import numpy as np
import ml_dtypes


def mxq(x, axis, fmt="e4m3"):
    dtype, down = {"e4m3": (ml_dtypes.float8_e4m3fn, 7), "e5m2": (ml_dtypes.float8_e5m2, 14)}[fmt]
    v = np.moveaxis(np.asarray(x, np.float32).astype(ml_dtypes.bfloat16).astype(np.float64), axis, -1)
    blocks = v.reshape(v.shape[:-1] + (-1, 32))
    amax = np.abs(blocks).max(-1, keepdims=True)
    byte = np.maximum(np.where(amax > 0, np.frexp(amax)[1] - 1 + 127, 0) - down, 1)
    scale = np.exp2(byte - 127.0)
    codes = (blocks / scale).astype(np.float32).astype(dtype).astype(np.float64)
    return np.moveaxis((codes * scale).reshape(v.shape), -1, axis)


WIDE = False


def mx_kscale(k):
    if not WIDE:
        return np.ones(k)
    levels = np.array([10, -10, 5, -5, 0])
    if k % 512:
        return np.exp2(np.random.permutation(np.resize(levels, k // 32))).repeat(32)
    a = np.empty((k // 512, 16))
    for p in range(k // 512):
        a[p, :8] = np.random.permutation(np.resize(levels, 8))
        for g in range(8):
            far = levels[np.abs(levels - a[p, g]) >= 10]
            a[p, g + 8] = far[np.random.randint(len(far))]
    return np.exp2(a.ravel()).repeat(32)


BF16 = ml_dtypes.bfloat16


def bf(x):
    return np.asarray(x, np.float32).astype(BF16)


def f64(x):
    return np.asarray(x).astype(np.float64)


B, NH, NW, C, K, P = 2, 16, 16, 1024, 256, 4
T = P * P
HAD = np.array([[1.0, 1.0, 1.0, 1.0],
                [1.0, -1.0, 1.0, -1.0],
                [1.0, 1.0, -1.0, -1.0],
                [1.0, -1.0, -1.0, 1.0]])


def setup_inputs():
    s = mx_kscale(C)
    return {"trans": bf(np.random.standard_normal((T, B, NH, NW, C)) * s),
            "weight": bf(np.random.standard_normal((T, C, K)) * 0.5 * P / np.sqrt(C) / s[:, None]),
            "bias": bf(np.random.standard_normal((1, 1, 1, K)) * 0.2)}


def reference(trans, weight, bias):
    x = f64(trans).reshape(T, B * NH * NW, C)
    y = mxq(x, 2, "e4m3") @ mxq(f64(weight), 1, "e4m3")
    y = y.reshape(P, P, B, NH, NW, K)
    r = np.stack([sum(HAD[p, u] * y[u] for u in range(P)) for p in range(P)])
    z = np.stack([sum(HAD[q, v] * r[:, v] for v in range(P)) for q in range(P)], axis=1) / T
    z = z.transpose(2, 3, 0, 4, 1, 5)
    return z.reshape(B, P * NH, P * NW, K) + f64(bias)

@@ -1,0 +1,247 @@
+from contextlib import ExitStack
+
+import concourse.mybir as mybir
+from concourse.masks import make_identity
+
+F32 = mybir.dt.float32
+BF16 = mybir.dt.bfloat16
+U32 = mybir.dt.uint32
+U8 = mybir.dt.uint8
+FP8X4 = mybir.dt.float8_e4m3fn_x4
+ALU = mybir.AluOpType
+
+P = 128
+N_OUT = 256
+STEPS = 16
+FLOPS = 2 * 16 * 512 * 1024 * 256
+
+PLUS = {1: (0, 2), 2: (0, 1), 3: (0, 3)}
+
+
+def tile_iwht3layer_pa_t_kernel(tc, trans, weight, bias, out):
+    nc = tc.nc
+    x_view = trans.rearrange("t b i (jj s) c -> (b i jj) t s c", s=4)
+    w_view = weight.rearrange("t (g q j) n -> q t g (j n)", g=2, q=P, j=4)
+    o_view = out.rearrange("b (i pp) (jj s q) n -> (b i) pp jj s (q n)", pp=4, jj=4, s=4, q=4)
+
+    with ExitStack() as ctx:
+        const = ctx.enter_context(tc.tile_pool(name="const", bufs=1))
+        wq_pool = ctx.enter_context(tc.tile_pool(name="wq", bufs=1))
+        wraw_pool = ctx.enter_context(tc.tile_pool(name="wraw", bufs=8))
+        wgrp_pool = ctx.enter_context(tc.tile_pool(name="wgrp", bufs=2))
+        xraw_pool = ctx.enter_context(tc.tile_pool(name="xraw", bufs=5))
+        xgrp_pool = ctx.enter_context(tc.tile_pool(name="xgrp", bufs=2))
+        xq_pool = ctx.enter_context(tc.tile_pool(name="xq", bufs=3))
+        r_pool = ctx.enter_context(tc.tile_pool(name="r", bufs=2))
+        am_pool = ctx.enter_context(tc.tile_pool(name="am", bufs=2))
+        z_pool = ctx.enter_context(tc.tile_pool(name="z", bufs=2))
+        ps_t = ctx.enter_context(tc.psum_pool(name="pst", bufs=4))
+        ps_a = ctx.enter_context(tc.psum_pool(name="psa", bufs=4))
+        ctx.enter_context(tc.manual_schedule())
+
+        ident = const.tile([P, P], F32)
+        make_identity(nc, ident[:])
+        bias_bc = const.tile([P, N_OUT], BF16)
+        nc.scalar.dma_start(out=bias_bc[:], in_=bias.rearrange("a b c n -> (a b c n)").partition_broadcast(P))
+        bias_f = const.tile([P, N_OUT], F32)
+        nc.gpsimd.tensor_copy(out=bias_f[:], in_=bias_bc[:])
+        wc = wq_pool.tile([P, 16 * 512], U32, align_bytes=64)
+        ws = wq_pool.tile([P, 16 * 512], U8, align_bytes=64)
+
+        xraw = {}
+        wraw = {}
+        xts = {}
+        xgrp = {}
+        xcs = {}
+        banks = {}
+        rs = {}
+        zs = {}
+
+        def load_x(k):
+            s, u = divmod(k, 4)
+            xr = xraw_pool.tile([P, 4096], BF16)
+            nc.sync.dma_start(out=xr[:].rearrange("p (v c) -> p v c", v=4), in_=x_view[:, 4 * u : 4 * u + 4, s, :])
+            xraw[k] = xr
+
+        def load_w(u):
+            for t in range(4 * u, 4 * u + 4):
+                wr = wraw_pool.tile([P, 2048], BF16)
+                nc.sync.dma_start(out=wr[:].rearrange("q (g m) -> q g m", g=2), in_=w_view[:, t, :, :])
+                wraw[t] = wr
+
+        def transposes(k):
+            xw = xraw[k][:].bitcast(F32)
+            tiles = []
+            for v in range(4):
+                xt = ps_t.tile([P, 512], F32)
+                for a in range(4):
+                    g, h = divmod(a, 2)
+                    first = 512 * v + 256 * g
+                    nc.tensor.transpose(xt[:, P * a : P * a + P], xw[:, first + h : first + 256 : 2], ident[:])
+                tiles.append(xt)
+            xts[k] = tiles
+
+        def evacuate(k):
+            xg = xgrp_pool.tile([P, 4096], BF16, align_bytes=64)
+            xgw = xg[:].bitcast(F32)
+            for v in range(4):
+                nc.scalar.copy(
+                    out=xgw[:, 512 * v : 512 * v + 512].rearrange("q (g p u) -> q g p u", g=2, p=P, u=2),
+                    in_=xts[k][v][:].rearrange("q (g u p) -> q g p u", g=2, u=2, p=P),
+                )
+            xgrp[k] = xg
+
+        def quantise_x(k):
+            xc = xq_pool.tile([P, 1024], U32, align_bytes=64)
+            xs = xq_pool.tile([P, 1024], U8, align_bytes=64)
+            nc.vector.quantize_mx(out=xc[:].bitcast(FP8X4), scales=xs[:], in_=xgrp[k][:])
+            xcs[k] = (xc, xs)
+
+        def weights(u):
+            pending = None
+            for half in range(2):
+                wg = wgrp_pool.tile([P, 4096], BF16, align_bytes=64)
+                t = 4 * u + 2 * half
+                for g in range(2):
+                    nc.scalar.copy(
+                        out=wg[:, 1024 * g : 1024 * g + 1024].rearrange("q (c i j) -> q c j i", c=64, i=4, j=4),
+                        in_=wraw[t][:, 1024 * g : 1024 * g + 1024].rearrange("q (j c i) -> q c j i", j=4, c=64, i=4),
+                    )
+                nc.vector.tensor_copy(
+                    out=wg[:, 2048:4096].rearrange("q (g c i j) -> q g c j i", g=2, c=64, i=4, j=4),
+                    in_=wraw[t + 1][:].rearrange("q (g j c i) -> q g c j i", g=2, j=4, c=64, i=4),
+                )
+                if pending is not None:
+                    quantise_w(pending[0], pending[1])
+                pending = (2 * u + half, wg)
+            quantise_w(pending[0], pending[1])
+
+        def quantise_w(pair, wg):
+            nc.vector.quantize_mx(
+                out=wc[:, 1024 * pair : 1024 * pair + 1024].bitcast(FP8X4), scales=ws[:, 1024 * pair : 1024 * pair + 1024], in_=wg[:]
+            )
+
+        def sums(k):
+            u = k % 4
+            xc, xs = xcs[k]
+            bank_x = ps_a.tile([P, 512], F32, tag="acc")
+            bank_y = ps_a.tile([P, 512], F32, tag="acc")
+            jobs = [(bank_x, 0, (0, 1, 2, 3)), (bank_x, 1, PLUS[1]), (bank_y, 0, PLUS[2]), (bank_y, 1, PLUS[3])]
+            for bank, half, members in jobs:
+                passes = [(v, g) for v in members for g in range(2)]
+                for i, (v, g) in enumerate(passes):
+                    xo = (2 * v + g) * P
+                    wo = (2 * (4 * u + v) + g) * N_OUT
+                    nc.tensor.matmul_mx(
+                        out=bank[:, N_OUT * half : N_OUT * half + N_OUT],
+                        lhsT=xc[:, xo : xo + P].bitcast(FP8X4),
+                        lhsT_scale=xs[:, xo : xo + P],
+                        rhs=wc[:, wo : wo + N_OUT].bitcast(FP8X4),
+                        rhs_scale=ws[:, wo : wo + N_OUT],
+                        start=(i == 0),
+                        stop=(i == len(passes) - 1),
+                    )
+            banks[k] = (bank_x, bank_y)
+
+        def halves(ap):
+            return ap.rearrange("p (h n) -> p h n", h=2)
+
+        def level1(k):
+            s, u = divmod(k, 4)
+            bank_x, bank_y = banks[k]
+            if u == 0:
+                r_new = r_pool.tile([P, 4096], F32)
+                rs[s] = r_new
+            r = rs[s][:, 1024 * u : 1024 * u + 1024]
+            nc.scalar.mul(out=r[:, 0:N_OUT], in_=bank_x[:, 0:N_OUT], mul=1.0 / 16.0)
+            base = r[:, 0:N_OUT]
+            if u == 0:
+                am = am_pool.tile([P, N_OUT], F32)
+                nc.gpsimd.tensor_tensor(out=am[:], in0=r[:, 0:N_OUT], in1=bias_f[:], op=ALU.subtract)
+                nc.gpsimd.tensor_tensor(out=r[:, 0:N_OUT], in0=r[:, 0:N_OUT], in1=bias_f[:], op=ALU.add)
+                base = am[:]
+            nc.vector.scalar_tensor_tensor(
+                out=r[:, N_OUT:512], in0=bank_x[:, N_OUT:512], scalar=0.125, in1=base, op0=ALU.mult, op1=ALU.subtract
+            )
+            nc.vector.scalar_tensor_tensor(
+                out=halves(r[:, 512:1024]), in0=halves(bank_y[:]), scalar=0.125,
+                in1=base.unsqueeze(1).to_broadcast([P, 2, N_OUT]), op0=ALU.mult, op1=ALU.subtract,
+            )
+
+        def pair_stage(s, h):
+            if h == 0:
+                z_new = z_pool.tile([P, 4096], F32)
+                zs[s] = z_new
+            lo = 2048 * h
+            r = rs[s]
+            z = zs[s]
+            nc.vector.tensor_tensor(out=z[:, lo : lo + 1024], in0=r[:, lo : lo + 1024], in1=r[:, lo + 1024 : lo + 2048], op=ALU.add)
+            nc.vector.tensor_tensor(
+                out=z[:, lo + 1024 : lo + 2048], in0=r[:, lo : lo + 1024], in1=r[:, lo + 1024 : lo + 2048], op=ALU.subtract
+            )
+
+        def finish(s, h):
+            r = rs[s]
+            z = zs[s]
+            parts = 2 if (s, h) == (3, 1) else 1
+            rows = 2 // parts
+            for part in range(parts):
+                zo = 1024 * rows * part
+                lo = 2048 * h + zo
+                nc.vector.tensor_tensor(
+                    out=r[:, lo : lo + 1024 * rows], in0=z[:, zo : zo + 1024 * rows], in1=z[:, 2048 + zo : 2048 + zo + 1024 * rows],
+                    op=(ALU.add if h == 0 else ALU.subtract),
+                )
+                pp = 2 * h + rows * part
+                for jj in range(4):
+                    nc.sync.dma_start(
+                        out=o_view[:, pp : pp + rows, jj, s, :],
+                        in_=r[jj:P:4, lo : lo + 1024 * rows].rearrange("p (m c) -> p m c", m=rows),
+                    )
+
+        later = []
+        served = [0]
+
+        def second_level():
+            if served[0] < len(later):
+                job = later[served[0]]
+                served[0] += 1
+                job[0](job[1], job[2])
+
+        load_x(0)
+        load_w(0)
+        load_x(1)
+        load_w(1)
+        load_x(2)
+        transposes(0)
+        evacuate(0)
+        quantise_x(0)
+        weights(0)
+        load_w(2)
+        load_x(3)
+        for k in range(STEPS):
+            s, u = divmod(k, 4)
+            nxt = k + 1
+            if nxt < STEPS:
+                transposes(nxt)
+                evacuate(nxt)
+                quantise_x(nxt)
+            sums(k)
+            if nxt < 4:
+                weights(nxt)
+            if nxt == 1:
+                load_w(3)
+                load_x(4)
+            level1(k)
+            if u == 1:
+                later.append((pair_stage, s, 0))
+            if u == 3:
+                later.append((pair_stage, s, 1))
+                later.append((finish, s, 0))
+                later.append((finish, s, 1))
+            if k >= 1:
+                second_level()
+            if nxt + 4 < STEPS:
+                load_x(nxt + 4)
+        for i in range(len(later) - served[0]):
+            second_level()

@@ -13,9 +13,12 @@ ALU = mybir.AluOpType
 P = 128
 N_OUT = 256
 STEPS = 16
+X_BUFS = 5
+W_BUFS = 6
 FLOPS = 2 * 16 * 512 * 1024 * 256
 
 PLUS = {1: (0, 2), 2: (0, 1), 3: (0, 3)}
+ORDER = [(s, u) for u in range(4) for s in (0, 1)] + [(s, u) for s in (2, 3) for u in range(4)]
 
 
 def tile_iwht3layer_pa_t_kernel(tc, trans, weight, bias, out):
@@ -27,12 +30,12 @@ def tile_iwht3layer_pa_t_kernel(tc, trans, weight, bias, out):
     with ExitStack() as ctx:
         const = ctx.enter_context(tc.tile_pool(name="const", bufs=1))
         wq_pool = ctx.enter_context(tc.tile_pool(name="wq", bufs=1))
-        wraw_pool = ctx.enter_context(tc.tile_pool(name="wraw", bufs=8))
+        wraw_pool = ctx.enter_context(tc.tile_pool(name="wraw", bufs=W_BUFS))
         wgrp_pool = ctx.enter_context(tc.tile_pool(name="wgrp", bufs=2))
-        xraw_pool = ctx.enter_context(tc.tile_pool(name="xraw", bufs=5))
+        xraw_pool = ctx.enter_context(tc.tile_pool(name="xraw", bufs=X_BUFS))
         xgrp_pool = ctx.enter_context(tc.tile_pool(name="xgrp", bufs=2))
         xq_pool = ctx.enter_context(tc.tile_pool(name="xq", bufs=3))
-        r_pool = ctx.enter_context(tc.tile_pool(name="r", bufs=2))
+        r_pool = ctx.enter_context(tc.tile_pool(name="r", bufs=3))
         am_pool = ctx.enter_context(tc.tile_pool(name="am", bufs=2))
         z_pool = ctx.enter_context(tc.tile_pool(name="z", bufs=2))
         ps_t = ctx.enter_context(tc.psum_pool(name="pst", bufs=4))
@@ -50,46 +53,46 @@ def tile_iwht3layer_pa_t_kernel(tc, trans, weight, bias, out):
 
         xraw = {}
         wraw = {}
-        xts = {}
         xgrp = {}
         xcs = {}
         banks = {}
         rs = {}
         zs = {}
+        wgs = {}
 
         def load_x(k):
-            s, u = divmod(k, 4)
+            s, u = ORDER[k]
             xr = xraw_pool.tile([P, 4096], BF16)
             nc.sync.dma_start(out=xr[:].rearrange("p (v c) -> p v c", v=4), in_=x_view[:, 4 * u : 4 * u + 4, s, :])
             xraw[k] = xr
 
-        def load_w(u):
-            for t in range(4 * u, 4 * u + 4):
-                wr = wraw_pool.tile([P, 2048], BF16)
-                nc.sync.dma_start(out=wr[:].rearrange("q (g m) -> q g m", g=2), in_=w_view[:, t, :, :])
-                wraw[t] = wr
+        def load_w(t):
+            wr = wraw_pool.tile([P, 2048], BF16)
+            nc.sync.dma_start(out=wr[:].rearrange("q (g m) -> q g m", g=2), in_=w_view[:, t, :, :])
+            wraw[t] = wr
 
-        def transposes(k):
+        def turn(k, half):
+            if half == 0:
+                xg = xgrp_pool.tile([P, 4096], BF16, align_bytes=64)
+                xgrp[k] = xg
             xw = xraw[k][:].bitcast(F32)
+            xgw = xgrp[k][:].bitcast(F32)
             tiles = []
-            for v in range(4):
+            for v in (2 * half, 2 * half + 1):
                 xt = ps_t.tile([P, 512], F32)
                 for a in range(4):
                     g, h = divmod(a, 2)
                     first = 512 * v + 256 * g
                     nc.tensor.transpose(xt[:, P * a : P * a + P], xw[:, first + h : first + 256 : 2], ident[:])
-                tiles.append(xt)
-            xts[k] = tiles
-
-        def evacuate(k):
-            xg = xgrp_pool.tile([P, 4096], BF16, align_bytes=64)
-            xgw = xg[:].bitcast(F32)
-            for v in range(4):
+                tiles.append((v, xt))
+            if half == 1:
+                used["x"] += 1
+                loads()
+            for v, xt in tiles:
                 nc.scalar.copy(
                     out=xgw[:, 512 * v : 512 * v + 512].rearrange("q (g p u) -> q g p u", g=2, p=P, u=2),
-                    in_=xts[k][v][:].rearrange("q (g u p) -> q g p u", g=2, u=2, p=P),
+                    in_=xt[:].rearrange("q (g u p) -> q g p u", g=2, u=2, p=P),
                 )
-            xgrp[k] = xg
 
         def quantise_x(k):
             xc = xq_pool.tile([P, 1024], U32, align_bytes=64)
@@ -97,37 +100,32 @@ def tile_iwht3layer_pa_t_kernel(tc, trans, weight, bias, out):
             nc.vector.quantize_mx(out=xc[:].bitcast(FP8X4), scales=xs[:], in_=xgrp[k][:])
             xcs[k] = (xc, xs)
 
-        def weights(u):
-            pending = None
-            for half in range(2):
-                wg = wgrp_pool.tile([P, 4096], BF16, align_bytes=64)
-                t = 4 * u + 2 * half
-                for g in range(2):
-                    nc.scalar.copy(
-                        out=wg[:, 1024 * g : 1024 * g + 1024].rearrange("q (c i j) -> q c j i", c=64, i=4, j=4),
-                        in_=wraw[t][:, 1024 * g : 1024 * g + 1024].rearrange("q (j c i) -> q c j i", j=4, c=64, i=4),
-                    )
-                nc.vector.tensor_copy(
-                    out=wg[:, 2048:4096].rearrange("q (g c i j) -> q g c j i", g=2, c=64, i=4, j=4),
-                    in_=wraw[t + 1][:].rearrange("q (g j c i) -> q g c j i", g=2, j=4, c=64, i=4),
+        def regroup(pair):
+            wg = wgrp_pool.tile([P, 4096], BF16, align_bytes=64)
+            for g in range(2):
+                nc.scalar.copy(
+                    out=wg[:, 1024 * g : 1024 * g + 1024].rearrange("q (c i j) -> q c j i", c=64, i=4, j=4),
+                    in_=wraw[2 * pair][:, 1024 * g : 1024 * g + 1024].rearrange("q (j c i) -> q c j i", j=4, c=64, i=4),
                 )
-                if pending is not None:
-                    quantise_w(pending[0], pending[1])
-                pending = (2 * u + half, wg)
-            quantise_w(pending[0], pending[1])
+            nc.vector.tensor_copy(
+                out=wg[:, 2048:4096].rearrange("q (g c i j) -> q g c j i", g=2, c=64, i=4, j=4),
+                in_=wraw[2 * pair + 1][:].rearrange("q (g j c i) -> q g c j i", g=2, j=4, c=64, i=4),
+            )
+            wgs[pair] = wg
+            used["w"] += 2
+            loads()
 
-        def quantise_w(pair, wg):
+        def quantise_w(pair):
             nc.vector.quantize_mx(
-                out=wc[:, 1024 * pair : 1024 * pair + 1024].bitcast(FP8X4), scales=ws[:, 1024 * pair : 1024 * pair + 1024], in_=wg[:]
+                out=wc[:, 1024 * pair : 1024 * pair + 1024].bitcast(FP8X4),
+                scales=ws[:, 1024 * pair : 1024 * pair + 1024],
+                in_=wgs[pair][:],
             )
 
-        def sums(k):
-            u = k % 4
+        def sums(k, bank, jobs):
+            u = ORDER[k][1]
             xc, xs = xcs[k]
-            bank_x = ps_a.tile([P, 512], F32, tag="acc")
-            bank_y = ps_a.tile([P, 512], F32, tag="acc")
-            jobs = [(bank_x, 0, (0, 1, 2, 3)), (bank_x, 1, PLUS[1]), (bank_y, 0, PLUS[2]), (bank_y, 1, PLUS[3])]
-            for bank, half, members in jobs:
+            for half, members in enumerate(jobs):
                 passes = [(v, g) for v in members for g in range(2)]
                 for i, (v, g) in enumerate(passes):
                     xo = (2 * v + g) * P
@@ -141,25 +139,36 @@ def tile_iwht3layer_pa_t_kernel(tc, trans, weight, bias, out):
                         start=(i == 0),
                         stop=(i == len(passes) - 1),
                     )
-            banks[k] = (bank_x, bank_y)
 
         def halves(ap):
             return ap.rearrange("p (h n) -> p h n", h=2)
 
-        def level1(k):
-            s, u = divmod(k, 4)
-            bank_x, bank_y = banks[k]
-            if u == 0:
+        def sums_x(k):
+            s, u = ORDER[k]
+            bank = ps_a.tile([P, 512], F32, tag="acc")
+            sums(k, bank, ((0, 1, 2, 3), PLUS[1]))
+            if s not in rs:
                 r_new = r_pool.tile([P, 4096], F32)
                 rs[s] = r_new
             r = rs[s][:, 1024 * u : 1024 * u + 1024]
-            nc.scalar.mul(out=r[:, 0:N_OUT], in_=bank_x[:, 0:N_OUT], mul=1.0 / 16.0)
+            nc.scalar.mul(out=r[:, 0:N_OUT], in_=bank[:, 0:N_OUT], mul=1.0 / 16.0)
             base = r[:, 0:N_OUT]
             if u == 0:
                 am = am_pool.tile([P, N_OUT], F32)
                 nc.gpsimd.tensor_tensor(out=am[:], in0=r[:, 0:N_OUT], in1=bias_f[:], op=ALU.subtract)
                 nc.gpsimd.tensor_tensor(out=r[:, 0:N_OUT], in0=r[:, 0:N_OUT], in1=bias_f[:], op=ALU.add)
                 base = am[:]
+            banks[k] = [bank, base]
+
+        def sums_y(k):
+            bank = ps_a.tile([P, 512], F32, tag="acc")
+            sums(k, bank, (PLUS[2], PLUS[3]))
+            banks[k].append(bank)
+
+        def level1(k):
+            s, u = ORDER[k]
+            bank_x, base, bank_y = banks[k]
+            r = rs[s][:, 1024 * u : 1024 * u + 1024]
             nc.vector.scalar_tensor_tensor(
                 out=r[:, N_OUT:512], in0=bank_x[:, N_OUT:512], scalar=0.125, in1=base, op0=ALU.mult, op1=ALU.subtract
             )
@@ -208,30 +217,46 @@ def tile_iwht3layer_pa_t_kernel(tc, trans, weight, bias, out):
                 served[0] += 1
                 job[0](job[1], job[2])
 
-        load_x(0)
-        load_w(0)
-        load_x(1)
-        load_w(1)
-        load_x(2)
-        transposes(0)
-        evacuate(0)
+        queue = [("x", 0), ("w", 0), ("w", 1), ("w", 2), ("w", 3), ("x", 1)]
+        for u in range(1, 4):
+            queue += [("w", 4 * u), ("w", 4 * u + 1), ("x", 2 * u), ("w", 4 * u + 2), ("w", 4 * u + 3), ("x", 2 * u + 1)]
+        queue += [("x", k) for k in range(8, STEPS)]
+        issued = {"x": 0, "w": 0}
+        used = {"x": 0, "w": 0}
+
+        def loads():
+            while queue:
+                kind, i = queue[0]
+                if issued[kind] - used[kind] >= (X_BUFS if kind == "x" else W_BUFS):
+                    return
+                queue.pop(0)
+                issued[kind] += 1
+                (load_x if kind == "x" else load_w)(i)
+
+        loads()
+        turn(0, 0)
+        turn(0, 1)
         quantise_x(0)
-        weights(0)
-        load_w(2)
-        load_x(3)
+        regroup(0)
+        regroup(1)
+        quantise_w(0)
+        turn(1, 0)
+        quantise_w(1)
         for k in range(STEPS):
-            s, u = divmod(k, 4)
-            nxt = k + 1
-            if nxt < STEPS:
-                transposes(nxt)
-                evacuate(nxt)
-                quantise_x(nxt)
-            sums(k)
-            if nxt < 4:
-                weights(nxt)
-            if nxt == 1:
-                load_w(3)
-                load_x(4)
+            s, u = ORDER[k]
+            ahead = k < 6
+            if k + 1 < STEPS:
+                turn(k + 1, 1)
+            if ahead:
+                regroup(k + 2)
+            if k + 1 < STEPS:
+                quantise_x(k + 1)
+            sums_x(k)
+            if k + 2 < STEPS:
+                turn(k + 2, 0)
+            sums_y(k)
+            if ahead:
+                quantise_w(k + 2)
             level1(k)
             if u == 1:
                 later.append((pair_stage, s, 0))
@@ -241,7 +266,7 @@ def tile_iwht3layer_pa_t_kernel(tc, trans, weight, bias, out):
                 later.append((finish, s, 1))
             if k >= 1:
                 second_level()
-            if nxt + 4 < STEPS:
-                load_x(nxt + 4)
+                if len(later) - served[0] > 2:
+                    second_level()
         for i in range(len(later) - served[0]):
             second_level()

@@ -13,12 +13,17 @@ ALU = mybir.AluOpType
 P = 128
 N_OUT = 256
 STEPS = 16
-X_BUFS = 5
-W_BUFS = 6
 FLOPS = 2 * 16 * 512 * 1024 * 256
 
 PLUS = {1: (0, 2), 2: (0, 1), 3: (0, 3)}
-ORDER = [(s, u) for u in range(4) for s in (0, 1)] + [(s, u) for s in (2, 3) for u in range(4)]
+RAW_BUFS = 7
+ORDER = [(0, 0), (1, 0), (0, 1), (1, 1), (2, 0), (3, 0), (2, 1), (0, 2), (0, 3), (3, 1), (1, 2), (1, 3), (2, 2), (2, 3), (3, 2), (3, 3)]
+LOADS = ["x0", "w0", "w1", "x1", "w2", "x2", "w3", "x3", "x4", "w4", "x5", "w5", "x6", "w6", "x7", "w7"] + ["x" + str(k) for k in range(8, 16)]
+PIECES = {0: (6, 6), 3: (8, 8), 4: (9, 9, 10), 5: (10, 12, 12), 6: (14, 14)}
+FILL = (4, 5, -2, 7, 0, -3) + (0,) * 8 + (11, -4, 13, -5, -6, 15, 0, -7)
+HEAD = (0, 1, 100, -10, 3, 101, -11)
+SKIP = ()
+LEAN = (2, 3, 6, 9)
 
 
 def tile_iwht3layer_pa_t_kernel(tc, trans, weight, bias, out):
@@ -30,14 +35,13 @@ def tile_iwht3layer_pa_t_kernel(tc, trans, weight, bias, out):
     with ExitStack() as ctx:
         const = ctx.enter_context(tc.tile_pool(name="const", bufs=1))
         wq_pool = ctx.enter_context(tc.tile_pool(name="wq", bufs=1))
-        wraw_pool = ctx.enter_context(tc.tile_pool(name="wraw", bufs=W_BUFS))
-        wgrp_pool = ctx.enter_context(tc.tile_pool(name="wgrp", bufs=2))
-        xraw_pool = ctx.enter_context(tc.tile_pool(name="xraw", bufs=X_BUFS))
+        raw_pool = ctx.enter_context(tc.tile_pool(name="raw", bufs=RAW_BUFS))
+        stage_pool = ctx.enter_context(tc.tile_pool(name="stage", bufs=4))
         xgrp_pool = ctx.enter_context(tc.tile_pool(name="xgrp", bufs=2))
         xq_pool = ctx.enter_context(tc.tile_pool(name="xq", bufs=3))
         r_pool = ctx.enter_context(tc.tile_pool(name="r", bufs=3))
         am_pool = ctx.enter_context(tc.tile_pool(name="am", bufs=2))
-        z_pool = ctx.enter_context(tc.tile_pool(name="z", bufs=2))
+        z_pool = ctx.enter_context(tc.tile_pool(name="z", bufs=6))
         ps_t = ctx.enter_context(tc.psum_pool(name="pst", bufs=4))
         ps_a = ctx.enter_context(tc.psum_pool(name="psa", bufs=4))
         ctx.enter_context(tc.manual_schedule())
@@ -48,35 +52,54 @@ def tile_iwht3layer_pa_t_kernel(tc, trans, weight, bias, out):
         nc.scalar.dma_start(out=bias_bc[:], in_=bias.rearrange("a b c n -> (a b c n)").partition_broadcast(P))
         bias_f = const.tile([P, N_OUT], F32)
         nc.gpsimd.tensor_copy(out=bias_f[:], in_=bias_bc[:])
+        bias_2 = const.tile([P, N_OUT], F32)
+        nc.gpsimd.tensor_tensor(out=bias_2[:], in0=bias_f[:], in1=bias_f[:], op=ALU.add)
         wc = wq_pool.tile([P, 16 * 512], U32, align_bytes=64)
         ws = wq_pool.tile([P, 16 * 512], U8, align_bytes=64)
 
-        xraw = {}
-        wraw = {}
+        raws = {}
+        readers = {}
+        free = [RAW_BUFS]
+        issued = []
+        queue = list(LOADS)
         xgrp = {}
+        xts = {}
         xcs = {}
         banks = {}
         rs = {}
         zs = {}
+        outs = {}
         wgs = {}
 
-        def load_x(k):
-            s, u = ORDER[k]
-            xr = xraw_pool.tile([P, 4096], BF16)
-            nc.sync.dma_start(out=xr[:].rearrange("p (v c) -> p v c", v=4), in_=x_view[:, 4 * u : 4 * u + 4, s, :])
-            xraw[k] = xr
+        def loads():
+            while queue and free[0]:
+                free[0] -= 1
+                name = queue.pop(0)
+                issued.append(name)
+                readers[name] = 2
+                raw = raw_pool.tile([P, 4096], BF16, tag="raw")
+                raws[name] = raw
+                if name[0] == "w":
+                    for i in range(2):
+                        part = raw[:, 2048 * i : 2048 * i + 2048]
+                        nc.sync.dma_start(out=part.rearrange("q (g m) -> q g m", g=2), in_=w_view[:, 2 * int(name[1]) + i, :, :])
+                else:
+                    s, u = ORDER[int(name[1:])]
+                    nc.sync.dma_start(out=raw[:].rearrange("p (v c) -> p v c", v=4), in_=x_view[:, 4 * u : 4 * u + 4, s, :])
 
-        def load_w(t):
-            wr = wraw_pool.tile([P, 2048], BF16)
-            nc.sync.dma_start(out=wr[:].rearrange("q (g m) -> q g m", g=2), in_=w_view[:, t, :, :])
-            wraw[t] = wr
+        def read(name):
+            readers[name] -= 1
+            while issued and readers[issued[0]] == 0:
+                issued.pop(0)
+                free[0] += 1
+            loads()
 
         def turn(k, half):
             if half == 0:
                 xg = xgrp_pool.tile([P, 4096], BF16, align_bytes=64)
                 xgrp[k] = xg
-            xw = xraw[k][:].bitcast(F32)
-            xgw = xgrp[k][:].bitcast(F32)
+            name = "x" + str(k)
+            xw = raws[name][:].bitcast(F32)
             tiles = []
             for v in (2 * half, 2 * half + 1):
                 xt = ps_t.tile([P, 512], F32)
@@ -85,10 +108,12 @@ def tile_iwht3layer_pa_t_kernel(tc, trans, weight, bias, out):
                     first = 512 * v + 256 * g
                     nc.tensor.transpose(xt[:, P * a : P * a + P], xw[:, first + h : first + 256 : 2], ident[:])
                 tiles.append((v, xt))
-            if half == 1:
-                used["x"] += 1
-                loads()
-            for v, xt in tiles:
+            xts[k, half] = tiles
+            read(name)
+
+        def copy_out(k, half):
+            xgw = xgrp[k][:].bitcast(F32)
+            for v, xt in xts[k, half]:
                 nc.scalar.copy(
                     out=xgw[:, 512 * v : 512 * v + 512].rearrange("q (g p u) -> q g p u", g=2, p=P, u=2),
                     in_=xt[:].rearrange("q (g u p) -> q g p u", g=2, u=2, p=P),
@@ -100,20 +125,29 @@ def tile_iwht3layer_pa_t_kernel(tc, trans, weight, bias, out):
             nc.vector.quantize_mx(out=xc[:].bitcast(FP8X4), scales=xs[:], in_=xgrp[k][:])
             xcs[k] = (xc, xs)
 
-        def regroup(pair):
-            wg = wgrp_pool.tile([P, 4096], BF16, align_bytes=64)
-            for g in range(2):
-                nc.scalar.copy(
-                    out=wg[:, 1024 * g : 1024 * g + 1024].rearrange("q (c i j) -> q c j i", c=64, i=4, j=4),
-                    in_=wraw[2 * pair][:, 1024 * g : 1024 * g + 1024].rearrange("q (j c i) -> q c j i", j=4, c=64, i=4),
-                )
-            nc.vector.tensor_copy(
-                out=wg[:, 2048:4096].rearrange("q (g c i j) -> q g c j i", g=2, c=64, i=4, j=4),
-                in_=wraw[2 * pair + 1][:].rearrange("q (g j c i) -> q g c j i", g=2, j=4, c=64, i=4),
+        def pair_tile(t):
+            if t // 2 not in wgs:
+                wg = stage_pool.tile([P, 4096], BF16, align_bytes=64, tag="stage")
+                wgs[t // 2] = wg
+            return wgs[t // 2][:, 2048 * (t % 2) : 2048 * (t % 2) + 2048]
+
+        def source(t):
+            return raws["w" + str(t // 2)][:, 2048 * (t % 2) : 2048 * (t % 2) + 2048]
+
+        def regroup_scalar(t, g):
+            nc.scalar.copy(
+                out=pair_tile(t)[:, 1024 * g : 1024 * g + 1024].rearrange("q (c i j) -> q c j i", c=64, i=4, j=4),
+                in_=source(t)[:, 1024 * g : 1024 * g + 1024].rearrange("q (j c i) -> q c j i", j=4, c=64, i=4),
             )
-            wgs[pair] = wg
-            used["w"] += 2
-            loads()
+            if g == 1:
+                read("w" + str(t // 2))
+
+        def regroup_vector(t):
+            nc.vector.tensor_copy(
+                out=pair_tile(t).rearrange("q (g c i j) -> q g c j i", g=2, c=64, i=4, j=4),
+                in_=source(t).rearrange("q (g j c i) -> q g c j i", g=2, j=4, c=64, i=4),
+            )
+            read("w" + str(t // 2))
 
         def quantise_w(pair):
             nc.vector.quantize_mx(
@@ -143,130 +177,174 @@ def tile_iwht3layer_pa_t_kernel(tc, trans, weight, bias, out):
         def halves(ap):
             return ap.rearrange("p (h n) -> p h n", h=2)
 
+        def part(k):
+            s, u = ORDER[k]
+            return rs[s, u // 2][:, 1024 * (u % 2) : 1024 * (u % 2) + 1024]
+
         def sums_x(k):
             s, u = ORDER[k]
             bank = ps_a.tile([P, 512], F32, tag="acc")
-            sums(k, bank, ((0, 1, 2, 3), PLUS[1]))
-            if s not in rs:
-                r_new = r_pool.tile([P, 4096], F32)
-                rs[s] = r_new
-            r = rs[s][:, 1024 * u : 1024 * u + 1024]
-            nc.scalar.mul(out=r[:, 0:N_OUT], in_=bank[:, 0:N_OUT], mul=1.0 / 16.0)
-            base = r[:, 0:N_OUT]
-            if u == 0:
+            sums(k, bank, (PLUS[1], (1, 3)) if k in LEAN else ((0, 1, 2, 3), PLUS[1]))
+            if u % 2 == 0:
+                r_new = r_pool.tile([P, 2048], F32)
+                rs[s, u // 2] = r_new
+            r = part(k)
+            if k in LEAN:
                 am = am_pool.tile([P, N_OUT], F32)
-                nc.gpsimd.tensor_tensor(out=am[:], in0=r[:, 0:N_OUT], in1=bias_f[:], op=ALU.subtract)
-                nc.gpsimd.tensor_tensor(out=r[:, 0:N_OUT], in0=r[:, 0:N_OUT], in1=bias_f[:], op=ALU.add)
-                base = am[:]
-            banks[k] = [bank, base]
+                nc.scalar.mul(out=am[:], in_=bank[:, 0:N_OUT], mul=1.0 / 16.0)
+                if u == 0:
+                    nc.gpsimd.tensor_tensor(out=am[:], in0=am[:], in1=bias_f[:], op=ALU.add)
+                banks[k] = [bank, am]
+                return
+            if u == 0:
+                banks[k] = [bank, None]
+                return
+            nc.scalar.mul(out=r[:, 0:N_OUT], in_=bank[:, 0:N_OUT], mul=1.0 / 16.0)
+            banks[k] = [bank, r[:, 0:N_OUT]]
 
         def sums_y(k):
             bank = ps_a.tile([P, 512], F32, tag="acc")
             sums(k, bank, (PLUS[2], PLUS[3]))
             banks[k].append(bank)
 
-        def level1(k):
-            s, u = ORDER[k]
-            bank_x, base, bank_y = banks[k]
-            r = rs[s][:, 1024 * u : 1024 * u + 1024]
-            nc.vector.scalar_tensor_tensor(
-                out=r[:, N_OUT:512], in0=bank_x[:, N_OUT:512], scalar=0.125, in1=base, op0=ALU.mult, op1=ALU.subtract
-            )
-            nc.vector.scalar_tensor_tensor(
-                out=halves(r[:, 512:1024]), in0=halves(bank_y[:]), scalar=0.125,
-                in1=base.unsqueeze(1).to_broadcast([P, 2, N_OUT]), op0=ALU.mult, op1=ALU.subtract,
-            )
-
-        def pair_stage(s, h):
-            if h == 0:
-                z_new = z_pool.tile([P, 4096], F32)
-                zs[s] = z_new
-            lo = 2048 * h
-            r = rs[s]
-            z = zs[s]
-            nc.vector.tensor_tensor(out=z[:, lo : lo + 1024], in0=r[:, lo : lo + 1024], in1=r[:, lo + 1024 : lo + 2048], op=ALU.add)
-            nc.vector.tensor_tensor(
-                out=z[:, lo + 1024 : lo + 2048], in0=r[:, lo : lo + 1024], in1=r[:, lo + 1024 : lo + 2048], op=ALU.subtract
-            )
-
-        def finish(s, h):
-            r = rs[s]
-            z = zs[s]
-            parts = 2 if (s, h) == (3, 1) else 1
-            rows = 2 // parts
-            for part in range(parts):
-                zo = 1024 * rows * part
-                lo = 2048 * h + zo
-                nc.vector.tensor_tensor(
-                    out=r[:, lo : lo + 1024 * rows], in0=z[:, zo : zo + 1024 * rows], in1=z[:, 2048 + zo : 2048 + zo + 1024 * rows],
-                    op=(ALU.add if h == 0 else ALU.subtract),
+        def level1_x(k):
+            if k in LEAN:
+                u = ORDER[k][1]
+                bank, am = banks[k]
+                for q, sign in ((0, 1.0), (1, -1.0)):
+                    nc.vector.scalar_tensor_tensor(
+                        out=part(k)[:, N_OUT * q : N_OUT * q + N_OUT], in0=bank[:, N_OUT:512], scalar=sign / 16.0, in1=am[:],
+                        op0=ALU.mult, op1=ALU.add,
+                    )
+                base = part(k)[:, 0:N_OUT]
+                if u == 0:
+                    less = am_pool.tile([P, N_OUT], F32)
+                    nc.gpsimd.tensor_tensor(out=less[:], in0=base, in1=bias_2[:], op=ALU.subtract)
+                    base = less[:]
+                banks[k][1] = base
+                return
+            if ORDER[k][1] == 0:
+                bank = banks[k][0]
+                am = am_pool.tile([P, N_OUT], F32)
+                nc.vector.scalar_tensor_tensor(
+                    out=am[:], in0=bank[:, 0:N_OUT], scalar=0.0625, in1=bias_f[:], op0=ALU.mult, op1=ALU.subtract
                 )
-                pp = 2 * h + rows * part
+                banks[k][1] = am[:]
+                nc.vector.scalar_tensor_tensor(
+                    out=halves(part(k)[:, 0:512]), in0=halves(bank[:]), scalar=0.125,
+                    in1=am[:].unsqueeze(1).to_broadcast([P, 2, N_OUT]), op0=ALU.mult, op1=ALU.subtract,
+                )
+                return
+            nc.vector.scalar_tensor_tensor(
+                out=part(k)[:, N_OUT:512], in0=banks[k][0][:, N_OUT:512], scalar=0.125, in1=banks[k][1],
+                op0=ALU.mult, op1=ALU.subtract,
+            )
+
+        def level1_y(k):
+            s, u = ORDER[k]
+            nc.vector.scalar_tensor_tensor(
+                out=halves(part(k)[:, 512:1024]), in0=halves(banks[k][2][:]), scalar=0.125,
+                in1=banks[k][1].unsqueeze(1).to_broadcast([P, 2, N_OUT]), op0=ALU.mult, op1=ALU.subtract,
+            )
+            if u % 2 == 1:
+                add, sub = [(pair_stage, s, u // 2, op) for op in (ALU.add, ALU.subtract)]
+                rows = [(finish, s, pp) for pp in (0, 2, 1, 3)] if u == 3 else []
+                later.extend([add] + rows[:2] + [sub] + rows[2:])
+
+        def combine(out_tile, lo, in0, lo0, in1, lo1, op):
+            nc.vector.tensor_tensor(
+                out=out_tile[:, lo : lo + 1024], in0=in0[:, lo0 : lo0 + 1024], in1=in1[:, lo1 : lo1 + 1024], op=op
+            )
+
+        def pair_stage(s, h, op):
+            if op == ALU.add:
+                z_new = z_pool.tile([P, 2048], F32)
+                zs[s, h] = z_new
+            combine(zs[s, h], 0 if op == ALU.add else 1024, rs[s, h], 0, rs[s, h], 1024, op)
+
+        def finish(s, pp):
+            if pp < 2:
+                o_new = stage_pool.tile([P, 2048], F32, align_bytes=64, tag="stage")
+                outs[s] = o_new
+            o = outs[s]
+            lo = 1024 * (pp // 2)
+            from_z = 1024 * (pp % 2)
+            combine(o, lo, zs[s, 0], from_z, zs[s, 1], from_z, ALU.add if pp < 2 else ALU.subtract)
+            if s == 3 or pp >= 2:
+                count = 1 if s == 3 else 2
+                first = pp if s == 3 else pp - 2
                 for jj in range(4):
                     nc.sync.dma_start(
-                        out=o_view[:, pp : pp + rows, jj, s, :],
-                        in_=r[jj:P:4, lo : lo + 1024 * rows].rearrange("p (m c) -> p m c", m=rows),
+                        out=o_view[:, first : pp + 1 : 2, jj, s, :],
+                        in_=o[jj:P:4, 1024 * (first // 2) : 1024 * (first // 2) + 1024 * count].rearrange("p (m c) -> p m c", m=count),
                     )
 
         later = []
-        served = [0]
 
         def second_level():
-            if served[0] < len(later):
-                job = later[served[0]]
-                served[0] += 1
-                job[0](job[1], job[2])
+            if later:
+                job = later.pop(0)
+                job[0](*job[1:])
 
-        queue = [("x", 0), ("w", 0), ("w", 1), ("w", 2), ("w", 3), ("x", 1)]
-        for u in range(1, 4):
-            queue += [("w", 4 * u), ("w", 4 * u + 1), ("x", 2 * u), ("w", 4 * u + 2), ("w", 4 * u + 3), ("x", 2 * u + 1)]
-        queue += [("x", k) for k in range(8, STEPS)]
-        issued = {"x": 0, "w": 0}
-        used = {"x": 0, "w": 0}
+        fill = list(FILL)
 
-        def loads():
-            while queue:
-                kind, i = queue[0]
-                if issued[kind] - used[kind] >= (X_BUFS if kind == "x" else W_BUFS):
-                    return
-                queue.pop(0)
-                issued[kind] += 1
-                (load_x if kind == "x" else load_w)(i)
+        def filler():
+            code = fill.pop(0) if fill else 0
+            if code > 0:
+                regroup_vector(code)
+            elif code < 0:
+                quantise_w(-code)
+            else:
+                second_level()
 
         loads()
         turn(0, 0)
+        copy_out(0, 0)
         turn(0, 1)
-        quantise_x(0)
-        regroup(0)
-        regroup(1)
-        quantise_w(0)
-        turn(1, 0)
-        quantise_w(1)
+        copy_out(0, 1)
+        for g in range(2):
+            regroup_scalar(2, g)
+        for code in HEAD:
+            if code == 100:
+                quantise_x(0)
+            elif code == 101:
+                turn(1, 0)
+                copy_out(1, 0)
+            elif code < 0:
+                quantise_w(-code - 10)
+            else:
+                regroup_vector(code)
+        done = {}
         for k in range(STEPS):
-            s, u = ORDER[k]
-            ahead = k < 6
+            mine = list(PIECES.get(k, ()))
+
+            def piece():
+                if mine:
+                    t = mine.pop(0)
+                    done[t] = done.get(t, -1) + 1
+                    regroup_scalar(t, done[t])
+
             if k + 1 < STEPS:
                 turn(k + 1, 1)
-            if ahead:
-                regroup(k + 2)
+                copy_out(k + 1, 1)
+            if k > 0:
+                piece()
+            if k >= 1:
+                level1_y(k - 1)
+            filler()
             if k + 1 < STEPS:
                 quantise_x(k + 1)
             sums_x(k)
+            filler()
+            level1_x(k)
             if k + 2 < STEPS:
                 turn(k + 2, 0)
+                copy_out(k + 2, 0)
+            piece()
+            piece()
             sums_y(k)
-            if ahead:
-                quantise_w(k + 2)
-            level1(k)
-            if u == 1:
-                later.append((pair_stage, s, 0))
-            if u == 3:
-                later.append((pair_stage, s, 1))
-                later.append((finish, s, 0))
-                later.append((finish, s, 1))
-            if k >= 1:
-                second_level()
-                if len(later) - served[0] > 2:
-                    second_level()
-        for i in range(len(later) - served[0]):
+            if k not in SKIP:
+                filler()
+        level1_y(STEPS - 1)
+        while later:
             second_level()

@@ -17,13 +17,14 @@ FLOPS = 2 * 16 * 512 * 1024 * 256
 
 PLUS = {1: (0, 2), 2: (0, 1), 3: (0, 3)}
 RAW_BUFS = 7
-ORDER = [(0, 0), (1, 0), (0, 1), (1, 1), (2, 0), (3, 0), (2, 1), (0, 2), (0, 3), (3, 1), (1, 2), (1, 3), (2, 2), (2, 3), (3, 2), (3, 3)]
-LOADS = ["x0", "w0", "w1", "x1", "w2", "x2", "w3", "x3", "x4", "w4", "x5", "w5", "x6", "w6", "x7", "w7"] + ["x" + str(k) for k in range(8, 16)]
-PIECES = {0: (6, 6), 3: (8, 8), 4: (9, 9, 10), 5: (10, 12, 12), 6: (14, 14)}
-FILL = (4, 5, -2, 7, 0, -3) + (0,) * 8 + (11, -4, 13, -5, -6, 15, 0, -7)
-HEAD = (0, 1, 100, -10, 3, 101, -11)
-SKIP = ()
-LEAN = (2, 3, 6, 9)
+ORDER = [(0, 0), (1, 0), (0, 1), (1, 1), (2, 0), (2, 1), (0, 2), (0, 3), (1, 2), (1, 3), (2, 2), (2, 3), (3, 0), (3, 1), (3, 2), (3, 3)]
+LOADS = ["x0", "w0", "w1", "x1", "w3", "x2", "w2", "x3", "w4", "x4", "w5", "x5", "w6", "x6", "w7", "x7"] + ["x" + str(k) for k in range(8, 16)]
+FILL = (7, 6, -3, -2, 0, 0, 8, 0, 0, 10, -4, 0, 0, -5, 0, 0, 0, -6, 0, -7)
+HEAD = (0, 1, 100, 3, -10, 101, -11)
+EARLY = {1: (5,), 2: (9,), 3: (11,), 4: (12,), 5: (13, 14), 6: (15,)}
+LATE = {0: (4, 4, 5), 2: (9,), 3: (11,), 4: (12, 13), 5: (14, 15)}
+THR = 2
+LEAN = (2, 3, 5, 6, 7, 8, 9)
 
 
 def tile_iwht3layer_pa_t_kernel(tc, trans, weight, bias, out):
@@ -52,8 +53,6 @@ def tile_iwht3layer_pa_t_kernel(tc, trans, weight, bias, out):
         nc.scalar.dma_start(out=bias_bc[:], in_=bias.rearrange("a b c n -> (a b c n)").partition_broadcast(P))
         bias_f = const.tile([P, N_OUT], F32)
         nc.gpsimd.tensor_copy(out=bias_f[:], in_=bias_bc[:])
-        bias_2 = const.tile([P, N_OUT], F32)
-        nc.gpsimd.tensor_tensor(out=bias_2[:], in0=bias_f[:], in1=bias_f[:], op=ALU.add)
         wc = wq_pool.tile([P, 16 * 512], U32, align_bytes=64)
         ws = wq_pool.tile([P, 16 * 512], U8, align_bytes=64)
 
@@ -192,12 +191,14 @@ def tile_iwht3layer_pa_t_kernel(tc, trans, weight, bias, out):
             if k in LEAN:
                 am = am_pool.tile([P, N_OUT], F32)
                 nc.scalar.mul(out=am[:], in_=bank[:, 0:N_OUT], mul=1.0 / 16.0)
-                if u == 0:
-                    nc.gpsimd.tensor_tensor(out=am[:], in0=am[:], in1=bias_f[:], op=ALU.add)
                 banks[k] = [bank, am]
                 return
             if u == 0:
-                banks[k] = [bank, None]
+                am = am_pool.tile([P, N_OUT], F32)
+                nc.vector.scalar_tensor_tensor(
+                    out=am[:], in0=bank[:, 0:N_OUT], scalar=0.0625, in1=bias_f[:], op0=ALU.mult, op1=ALU.subtract
+                )
+                banks[k] = [bank, am[:]]
                 return
             nc.scalar.mul(out=r[:, 0:N_OUT], in_=bank[:, 0:N_OUT], mul=1.0 / 16.0)
             banks[k] = [bank, r[:, 0:N_OUT]]
@@ -209,7 +210,6 @@ def tile_iwht3layer_pa_t_kernel(tc, trans, weight, bias, out):
 
         def level1_x(k):
             if k in LEAN:
-                u = ORDER[k][1]
                 bank, am = banks[k]
                 for q, sign in ((0, 1.0), (1, -1.0)):
                     nc.vector.scalar_tensor_tensor(
@@ -217,22 +217,13 @@ def tile_iwht3layer_pa_t_kernel(tc, trans, weight, bias, out):
                         op0=ALU.mult, op1=ALU.add,
                     )
                 base = part(k)[:, 0:N_OUT]
-                if u == 0:
-                    less = am_pool.tile([P, N_OUT], F32)
-                    nc.gpsimd.tensor_tensor(out=less[:], in0=base, in1=bias_2[:], op=ALU.subtract)
-                    base = less[:]
                 banks[k][1] = base
                 return
             if ORDER[k][1] == 0:
-                bank = banks[k][0]
-                am = am_pool.tile([P, N_OUT], F32)
-                nc.vector.scalar_tensor_tensor(
-                    out=am[:], in0=bank[:, 0:N_OUT], scalar=0.0625, in1=bias_f[:], op0=ALU.mult, op1=ALU.subtract
-                )
-                banks[k][1] = am[:]
+                bank, base = banks[k][0], banks[k][1]
                 nc.vector.scalar_tensor_tensor(
                     out=halves(part(k)[:, 0:512]), in0=halves(bank[:]), scalar=0.125,
-                    in1=am[:].unsqueeze(1).to_broadcast([P, 2, N_OUT]), op0=ALU.mult, op1=ALU.subtract,
+                    in1=base.unsqueeze(1).to_broadcast([P, 2, N_OUT]), op0=ALU.mult, op1=ALU.subtract,
                 )
                 return
             nc.vector.scalar_tensor_tensor(
@@ -249,7 +240,7 @@ def tile_iwht3layer_pa_t_kernel(tc, trans, weight, bias, out):
             if u % 2 == 1:
                 add, sub = [(pair_stage, s, u // 2, op) for op in (ALU.add, ALU.subtract)]
                 rows = [(finish, s, pp) for pp in (0, 2, 1, 3)] if u == 3 else []
-                later.extend([add] + rows[:2] + [sub] + rows[2:])
+                later.extend([add] + rows[:2] + [sub] + rows[2:] if s == 3 else [add, sub] + rows)
 
         def combine(out_tile, lo, in0, lo0, in1, lo1, op):
             nc.vector.tensor_tensor(
@@ -315,36 +306,34 @@ def tile_iwht3layer_pa_t_kernel(tc, trans, weight, bias, out):
             else:
                 regroup_vector(code)
         done = {}
+
+        def pieces(ts):
+            for t in ts:
+                done[t] = done.get(t, -1) + 1
+                regroup_scalar(t, done[t])
+
         for k in range(STEPS):
-            mine = list(PIECES.get(k, ()))
-
-            def piece():
-                if mine:
-                    t = mine.pop(0)
-                    done[t] = done.get(t, -1) + 1
-                    regroup_scalar(t, done[t])
-
             if k + 1 < STEPS:
                 turn(k + 1, 1)
                 copy_out(k + 1, 1)
-            if k > 0:
-                piece()
+            pieces(EARLY.get(k, ()))
             if k >= 1:
                 level1_y(k - 1)
             filler()
             if k + 1 < STEPS:
                 quantise_x(k + 1)
             sums_x(k)
-            filler()
+            if (fill and fill[0] != 0) or len(later) > THR:
+                filler()
+            elif fill:
+                fill.pop(0)
             level1_x(k)
             if k + 2 < STEPS:
                 turn(k + 2, 0)
                 copy_out(k + 2, 0)
-            piece()
-            piece()
+            pieces(LATE.get(k, ()))
             sums_y(k)
-            if k not in SKIP:
-                filler()
+            filler()
         level1_y(STEPS - 1)
         while later:
             second_level()

@@ -17,19 +17,19 @@ FLOPS = 2 * 16 * 512 * 1024 * 256
 
 PLUS = {1: (0, 2), 2: (0, 1), 3: (0, 3)}
 RAW_BUFS = 7
-ORDER = [(0, 0), (1, 0), (0, 1), (1, 1), (2, 0), (2, 1), (0, 2), (0, 3), (1, 2), (1, 3), (2, 2), (2, 3), (3, 0), (3, 1), (3, 2), (3, 3)]
-LOADS = ["x0", "w0", "w1", "x1", "w3", "x2", "w2", "x3", "w4", "x4", "w5", "x5", "w6", "x6", "w7", "x7"] + ["x" + str(k) for k in range(8, 16)]
-FILL = (7, 6, -3, -2, 0, 0, 8, 0, 0, 10, -4, 0, 0, -5, 0, 0, 0, -6, 0, -7)
+ORDER = [(0, 0), (1, 0), (0, 1), (1, 1), (2, 0), (3, 0), (2, 1), (3, 1)] + [(s, u) for s in range(4) for u in (2, 3)]
+LOADS = ["x0", "w0", "w1", "x1", "w2", "p100", "p110", "w3", "p001", "p011", "w4", "p101", "w5", "p111", "w6", "w7"] + ["p200", "p210", "p300", "p310", "p201", "p211", "p301", "p311"]
+FILL = (4, 5, -2, 6, -3, 0, 0, 0, 0, 8, 0, 0, 0, -4, 0, 0, -5, 0, 14, 0, 0, 0, -6, 0, -7)
 HEAD = (0, 1, 100, 3, -10, 101, -11)
-EARLY = {1: (5,), 2: (9,), 3: (11,), 4: (12,), 5: (13, 14), 6: (15,)}
-LATE = {0: (4, 4, 5), 2: (9,), 3: (11,), 4: (12, 13), 5: (14, 15)}
+EARLY = {1: (7, 7), 3: (9,), 4: (10,), 5: (11,), 6: (13,), 7: (15, 15)}
+LATE = {3: (9,), 4: (10, 11), 5: (12, 12), 6: (13,)}
 THR = 2
-LEAN = (2, 3, 5, 6, 7, 8, 9)
+LEAN = (2, 3, 6, 7, 8, 9)
 
 
 def tile_iwht3layer_pa_t_kernel(tc, trans, weight, bias, out):
     nc = tc.nc
-    x_view = trans.rearrange("t b i (jj s) c -> (b i jj) t s c", s=4)
+    x_view = trans.rearrange("t b i (jj s) c -> (b i jj) t (s c)", s=4)
     w_view = weight.rearrange("t (g q j) n -> q t g (j n)", g=2, q=P, j=4)
     o_view = out.rearrange("b (i pp) (jj s q) n -> (b i) pp jj s (q n)", pp=4, jj=4, s=4, q=4)
 
@@ -83,8 +83,16 @@ def tile_iwht3layer_pa_t_kernel(tc, trans, weight, bias, out):
                         part = raw[:, 2048 * i : 2048 * i + 2048]
                         nc.sync.dma_start(out=part.rearrange("q (g m) -> q g m", g=2), in_=w_view[:, 2 * int(name[1]) + i, :, :])
                 else:
-                    s, u = ORDER[int(name[1:])]
-                    nc.sync.dma_start(out=raw[:].rearrange("p (v c) -> p v c", v=4), in_=x_view[:, 4 * u : 4 * u + 4, s, :])
+                    if name[0] == "p":
+                        u, h, e = int(name[1]), int(name[2]), int(name[3])
+                        count, t, s = 2, 4 * u + 2 * h, 2 * e
+                    else:
+                        s, u = ORDER[int(name[1:])]
+                        count, t = 4, 4 * u
+                    width = 4096 // count
+                    nc.sync.dma_start(
+                        out=raw[:].rearrange("p (v m) -> p v m", v=count), in_=x_view[:, t : t + count, 1024 * s : 1024 * s + width]
+                    )
 
         def read(name):
             readers[name] -= 1
@@ -97,14 +105,16 @@ def tile_iwht3layer_pa_t_kernel(tc, trans, weight, bias, out):
             if half == 0:
                 xg = xgrp_pool.tile([P, 4096], BF16, align_bytes=64)
                 xgrp[k] = xg
-            name = "x" + str(k)
+            s, u = ORDER[k]
+            paired = k >= 2
+            name = "p" + str(u) + str(half) + str(s // 2) if paired else "x" + str(k)
             xw = raws[name][:].bitcast(F32)
             tiles = []
             for v in (2 * half, 2 * half + 1):
                 xt = ps_t.tile([P, 512], F32)
                 for a in range(4):
                     g, h = divmod(a, 2)
-                    first = 512 * v + 256 * g
+                    first = (1024 * (v % 2) + 512 * (s % 2) if paired else 512 * v) + 256 * g
                     nc.tensor.transpose(xt[:, P * a : P * a + P], xw[:, first + h : first + 256 : 2], ident[:])
                 tiles.append((v, xt))
             xts[k, half] = tiles

@@ -11,19 +11,32 @@ FP8X4 = mybir.dt.float8_e4m3fn_x4
 ALU = mybir.AluOpType
 
 P = 128
-N_OUT = 256
-STEPS = 16
-FLOPS = 2 * 16 * 512 * 1024 * 256
+C = 1024
+N = 256
+FLOPS = 2 * 16 * 512 * C * N
 
-PLUS = {1: (0, 2), 2: (0, 1), 3: (0, 3)}
-RAW_BUFS = 7
-ORDER = [(0, 0), (1, 0), (0, 1), (1, 1), (2, 0), (3, 0), (2, 1), (3, 1)] + [(s, u) for s in range(4) for u in (2, 3)]
-LOADS = ["x0", "w0", "w1", "x1", "w2", "p100", "p110", "w3", "p001", "p011", "w4", "p101", "w5", "p111", "w6", "w7"] + ["p200", "p210", "p300", "p310", "p201", "p211", "p301", "p311"]
-FILL = (4, 5, -2, 6, -3, 0, 0, 0, 0, 8, 0, 0, 0, -4, 0, 0, -5, 0, 14, 0, 0, 0, -6, 0, -7)
-HEAD = (0, 1, 100, 3, -10, 101, -11)
-EARLY = {1: (7, 7), 3: (9,), 4: (10,), 5: (11,), 6: (13,), 7: (15, 15)}
-LATE = {3: (9,), 4: (10, 11), 5: (12, 12), 6: (13,)}
-THR = 2
+PAIR = {1: (0, 2), 2: (0, 1), 3: (0, 3)}
+REST = (1, 3)
+
+ORDER = [(s, u) for pair in ((0, 1), (2, 3)) for u in (0, 1) for s in pair] + [(s, u) for s in range(4) for u in (2, 3)]
+STEPS = len(ORDER)
+
+LOADS = [("x", 0, 0, 0), ("x", 0, 1, 0), ("w", 0), ("w", 1), ("w", 2), ("x", 1, 0, 0), ("x", 1, 1, 0), ("w", 3)]
+FIRST_HALF = [("x", 0, 0, 1), ("x", 0, 1, 1), ("w", 4), ("x", 1, 0, 1), ("w", 5), ("x", 1, 1, 1), ("w", 6), ("w", 7)]
+SECOND_HALF = [("x", u, half, pair) for pair in range(2) for u in (2, 3) for half in range(2)]
+LOAD_BUFFERS = 7
+
+SCALAR_T = (7, 9, 10, 11, 13, 14, 15)
+HALVES_BETWEEN = {1: 2, 3: 1, 4: 1, 5: 1, 6: 1, 7: 2}
+HALVES_AFTER = {3: 1, 4: 2, 5: 1, 6: 2}
+
+WEIGHT_WORK = {
+    (0, 0): ("regroup", 4), (0, 1): ("regroup", 5), (0, 2): ("quantise", 2), (1, 0): ("regroup", 6), (1, 1): ("quantise", 3),
+    (3, 0): ("regroup", 8), (4, 1): ("quantise", 4), (5, 1): ("quantise", 5), (6, 0): ("regroup", 12), (7, 1): ("quantise", 6),
+    (8, 0): ("quantise", 7),
+}
+WAITING = 2
+
 LEAN = (2, 3, 6, 7, 8, 9)
 
 
@@ -35,315 +48,306 @@ def tile_iwht3layer_pa_t_kernel(tc, trans, weight, bias, out):
 
     with ExitStack() as ctx:
         const = ctx.enter_context(tc.tile_pool(name="const", bufs=1))
-        wq_pool = ctx.enter_context(tc.tile_pool(name="wq", bufs=1))
-        raw_pool = ctx.enter_context(tc.tile_pool(name="raw", bufs=RAW_BUFS))
+        codes_pool = ctx.enter_context(tc.tile_pool(name="codes", bufs=1))
+        load_pool = ctx.enter_context(tc.tile_pool(name="load", bufs=LOAD_BUFFERS))
         stage_pool = ctx.enter_context(tc.tile_pool(name="stage", bufs=4))
-        xgrp_pool = ctx.enter_context(tc.tile_pool(name="xgrp", bufs=2))
+        turned_pool = ctx.enter_context(tc.tile_pool(name="turned", bufs=2))
         xq_pool = ctx.enter_context(tc.tile_pool(name="xq", bufs=3))
-        r_pool = ctx.enter_context(tc.tile_pool(name="r", bufs=3))
-        am_pool = ctx.enter_context(tc.tile_pool(name="am", bufs=2))
-        z_pool = ctx.enter_context(tc.tile_pool(name="z", bufs=6))
-        ps_t = ctx.enter_context(tc.psum_pool(name="pst", bufs=4))
-        ps_a = ctx.enter_context(tc.psum_pool(name="psa", bufs=4))
+        z_pool = ctx.enter_context(tc.tile_pool(name="z", bufs=3))
+        base_pool = ctx.enter_context(tc.tile_pool(name="base", bufs=2))
+        half_pool = ctx.enter_context(tc.tile_pool(name="half", bufs=6))
+        turn_psum = ctx.enter_context(tc.psum_pool(name="turn", bufs=4))
+        sum_psum = ctx.enter_context(tc.psum_pool(name="sum", bufs=4))
         ctx.enter_context(tc.manual_schedule())
 
         ident = const.tile([P, P], F32)
         make_identity(nc, ident[:])
-        bias_bc = const.tile([P, N_OUT], BF16)
-        nc.scalar.dma_start(out=bias_bc[:], in_=bias.rearrange("a b c n -> (a b c n)").partition_broadcast(P))
-        bias_f = const.tile([P, N_OUT], F32)
-        nc.gpsimd.tensor_copy(out=bias_f[:], in_=bias_bc[:])
-        wc = wq_pool.tile([P, 16 * 512], U32, align_bytes=64)
-        ws = wq_pool.tile([P, 16 * 512], U8, align_bytes=64)
+        bias_bf = const.tile([P, N], BF16)
+        nc.scalar.dma_start(out=bias_bf[:], in_=bias.rearrange("a b c n -> (a b c n)").partition_broadcast(P))
+        bias_f = const.tile([P, N], F32)
+        nc.gpsimd.tensor_copy(out=bias_f[:], in_=bias_bf[:])
+        w_codes = codes_pool.tile([P, 16 * 2 * N], U32, align_bytes=64)
+        w_scales = codes_pool.tile([P, 16 * 2 * N], U8, align_bytes=64)
 
-        raws = {}
+        loaded = {}
         readers = {}
-        free = [RAW_BUFS]
-        issued = []
-        queue = list(LOADS)
-        xgrp = {}
-        xts = {}
-        xcs = {}
+        outstanding = []
+        spare = [LOAD_BUFFERS]
+        to_load = LOADS + FIRST_HALF + SECOND_HALF
+        turned = {}
+        turned_psum = {}
+        x_codes = {}
+        grouped = {}
         banks = {}
-        rs = {}
         zs = {}
-        outs = {}
-        wgs = {}
+        halves = {}
+        rows = {}
+        waiting = []
 
-        def loads():
-            while queue and free[0]:
-                free[0] -= 1
-                name = queue.pop(0)
-                issued.append(name)
+        def issue_loads():
+            while to_load and spare[0]:
+                spare[0] -= 1
+                name = to_load.pop(0)
+                outstanding.append(name)
                 readers[name] = 2
-                raw = raw_pool.tile([P, 4096], BF16, tag="raw")
-                raws[name] = raw
+                raw = load_pool.tile([P, 4096], BF16)
+                loaded[name] = raw
                 if name[0] == "w":
                     for i in range(2):
-                        part = raw[:, 2048 * i : 2048 * i + 2048]
-                        nc.sync.dma_start(out=part.rearrange("q (g m) -> q g m", g=2), in_=w_view[:, 2 * int(name[1]) + i, :, :])
+                        nc.sync.dma_start(
+                            out=raw[:, 2048 * i : 2048 * i + 2048].rearrange("q (g m) -> q g m", g=2),
+                            in_=w_view[:, 2 * name[1] + i, :, :],
+                        )
                 else:
-                    if name[0] == "p":
-                        u, h, e = int(name[1]), int(name[2]), int(name[3])
-                        count, t, s = 2, 4 * u + 2 * h, 2 * e
-                    else:
-                        s, u = ORDER[int(name[1:])]
-                        count, t = 4, 4 * u
-                    width = 4096 // count
+                    u, half, pair = name[1:]
+                    t = 4 * u + 2 * half
                     nc.sync.dma_start(
-                        out=raw[:].rearrange("p (v m) -> p v m", v=count), in_=x_view[:, t : t + count, 1024 * s : 1024 * s + width]
+                        out=raw[:].rearrange("p (v m) -> p v m", v=2),
+                        in_=x_view[:, t : t + 2, 2 * C * pair : 2 * C * pair + 2 * C],
                     )
 
-        def read(name):
+        def read_once(name):
             readers[name] -= 1
-            while issued and readers[issued[0]] == 0:
-                issued.pop(0)
-                free[0] += 1
-            loads()
+            while outstanding and readers[outstanding[0]] == 0:
+                outstanding.pop(0)
+                spare[0] += 1
+            issue_loads()
 
-        def turn(k, half):
-            if half == 0:
-                xg = xgrp_pool.tile([P, 4096], BF16, align_bytes=64)
-                xgrp[k] = xg
+        def transpose(k, half):
             s, u = ORDER[k]
-            paired = k >= 2
-            name = "p" + str(u) + str(half) + str(s // 2) if paired else "x" + str(k)
-            xw = raws[name][:].bitcast(F32)
+            if half == 0:
+                xt = turned_pool.tile([P, 4096], BF16, align_bytes=64)
+                turned[k] = xt
+            name = ("x", u, half, s // 2)
+            words = loaded[name][:].bitcast(F32)
             tiles = []
-            for v in (2 * half, 2 * half + 1):
-                xt = ps_t.tile([P, 512], F32)
-                for a in range(4):
-                    g, h = divmod(a, 2)
-                    first = (1024 * (v % 2) + 512 * (s % 2) if paired else 512 * v) + 256 * g
-                    nc.tensor.transpose(xt[:, P * a : P * a + P], xw[:, first + h : first + 256 : 2], ident[:])
-                tiles.append((v, xt))
-            xts[k, half] = tiles
-            read(name)
+            for v in range(2):
+                bank = turn_psum.tile([P, 512], F32)
+                for g in range(2):
+                    first = 1024 * v + 512 * (s % 2) + 256 * g
+                    for e in range(2):
+                        lo = P * (2 * g + e)
+                        nc.tensor.transpose(bank[:, lo : lo + P], words[:, first + e : first + 256 : 2], ident[:])
+                tiles.append((2 * half + v, bank))
+            turned_psum[k, half] = tiles
+            read_once(name)
 
         def copy_out(k, half):
-            xgw = xgrp[k][:].bitcast(F32)
-            for v, xt in xts[k, half]:
+            words = turned[k][:].bitcast(F32)
+            for v, bank in turned_psum[k, half]:
                 nc.scalar.copy(
-                    out=xgw[:, 512 * v : 512 * v + 512].rearrange("q (g p u) -> q g p u", g=2, p=P, u=2),
-                    in_=xt[:].rearrange("q (g u p) -> q g p u", g=2, u=2, p=P),
+                    out=words[:, 512 * v : 512 * v + 512].rearrange("q (g r e) -> q g r e", g=2, r=P, e=2),
+                    in_=bank[:].rearrange("q (g e r) -> q g r e", g=2, e=2, r=P),
                 )
 
         def quantise_x(k):
-            xc = xq_pool.tile([P, 1024], U32, align_bytes=64)
-            xs = xq_pool.tile([P, 1024], U8, align_bytes=64)
-            nc.vector.quantize_mx(out=xc[:].bitcast(FP8X4), scales=xs[:], in_=xgrp[k][:])
-            xcs[k] = (xc, xs)
+            codes = xq_pool.tile([P, 1024], U32, align_bytes=64)
+            scales = xq_pool.tile([P, 1024], U8, align_bytes=64)
+            nc.vector.quantize_mx(out=codes[:].bitcast(FP8X4), scales=scales[:], in_=turned[k][:])
+            x_codes[k] = (codes, scales)
 
-        def pair_tile(t):
-            if t // 2 not in wgs:
-                wg = stage_pool.tile([P, 4096], BF16, align_bytes=64, tag="stage")
-                wgs[t // 2] = wg
-            return wgs[t // 2][:, 2048 * (t % 2) : 2048 * (t % 2) + 2048]
+        def regroup_target(t):
+            if t // 2 not in grouped:
+                pair_tile = stage_pool.tile([P, 4096], BF16, align_bytes=64, tag="stage")
+                grouped[t // 2] = pair_tile
+            return grouped[t // 2][:, 2048 * (t % 2) : 2048 * (t % 2) + 2048]
 
-        def source(t):
-            return raws["w" + str(t // 2)][:, 2048 * (t % 2) : 2048 * (t % 2) + 2048]
+        def regroup_source(t):
+            return loaded["w", t // 2][:, 2048 * (t % 2) : 2048 * (t % 2) + 2048]
 
-        def regroup_scalar(t, g):
+        def regroup_on_scalar(t, g):
+            lo = 1024 * g
             nc.scalar.copy(
-                out=pair_tile(t)[:, 1024 * g : 1024 * g + 1024].rearrange("q (c i j) -> q c j i", c=64, i=4, j=4),
-                in_=source(t)[:, 1024 * g : 1024 * g + 1024].rearrange("q (j c i) -> q c j i", j=4, c=64, i=4),
+                out=regroup_target(t)[:, lo : lo + 1024].rearrange("q (c i j) -> q c j i", c=64, i=4, j=4),
+                in_=regroup_source(t)[:, lo : lo + 1024].rearrange("q (j c i) -> q c j i", j=4, c=64, i=4),
             )
             if g == 1:
-                read("w" + str(t // 2))
+                read_once(("w", t // 2))
 
-        def regroup_vector(t):
+        def regroup(t):
             nc.vector.tensor_copy(
-                out=pair_tile(t).rearrange("q (g c i j) -> q g c j i", g=2, c=64, i=4, j=4),
-                in_=source(t).rearrange("q (g j c i) -> q g c j i", g=2, j=4, c=64, i=4),
+                out=regroup_target(t).rearrange("q (g c i j) -> q g c j i", g=2, c=64, i=4, j=4),
+                in_=regroup_source(t).rearrange("q (g j c i) -> q g c j i", g=2, j=4, c=64, i=4),
             )
-            read("w" + str(t // 2))
+            read_once(("w", t // 2))
 
-        def quantise_w(pair):
+        def quantise(k):
+            lo = 1024 * k
             nc.vector.quantize_mx(
-                out=wc[:, 1024 * pair : 1024 * pair + 1024].bitcast(FP8X4),
-                scales=ws[:, 1024 * pair : 1024 * pair + 1024],
-                in_=wgs[pair][:],
+                out=w_codes[:, lo : lo + 1024].bitcast(FP8X4), scales=w_scales[:, lo : lo + 1024], in_=grouped[k][:]
             )
 
-        def sums(k, bank, jobs):
+        def sum_up(k, bank, members):
             u = ORDER[k][1]
-            xc, xs = xcs[k]
-            for half, members in enumerate(jobs):
-                passes = [(v, g) for v in members for g in range(2)]
+            codes, scales = x_codes[k]
+            for side, vs in enumerate(members):
+                passes = [(v, g) for v in vs for g in range(2)]
                 for i, (v, g) in enumerate(passes):
-                    xo = (2 * v + g) * P
-                    wo = (2 * (4 * u + v) + g) * N_OUT
+                    xo = P * (2 * v + g)
+                    wo = N * (2 * (4 * u + v) + g)
                     nc.tensor.matmul_mx(
-                        out=bank[:, N_OUT * half : N_OUT * half + N_OUT],
-                        lhsT=xc[:, xo : xo + P].bitcast(FP8X4),
-                        lhsT_scale=xs[:, xo : xo + P],
-                        rhs=wc[:, wo : wo + N_OUT].bitcast(FP8X4),
-                        rhs_scale=ws[:, wo : wo + N_OUT],
+                        out=bank[:, N * side : N * side + N],
+                        lhsT=codes[:, xo : xo + P].bitcast(FP8X4),
+                        lhsT_scale=scales[:, xo : xo + P],
+                        rhs=w_codes[:, wo : wo + N].bitcast(FP8X4),
+                        rhs_scale=w_scales[:, wo : wo + N],
                         start=(i == 0),
                         stop=(i == len(passes) - 1),
                     )
 
-        def halves(ap):
-            return ap.rearrange("p (h n) -> p h n", h=2)
+        def by_two(ap):
+            return ap.rearrange("p (m n) -> p m n", m=2)
 
-        def part(k):
-            s, u = ORDER[k]
-            return rs[s, u // 2][:, 1024 * (u % 2) : 1024 * (u % 2) + 1024]
+        def twice(ap):
+            return ap.unsqueeze(1).to_broadcast([P, 2, N])
 
-        def sums_x(k):
+        def z_of(k):
             s, u = ORDER[k]
-            bank = ps_a.tile([P, 512], F32, tag="acc")
-            sums(k, bank, (PLUS[1], (1, 3)) if k in LEAN else ((0, 1, 2, 3), PLUS[1]))
+            return zs[s, u // 2][:, 4 * N * (u % 2) : 4 * N * (u % 2) + 4 * N]
+
+        def first_sums(k):
+            s, u = ORDER[k]
+            bank = sum_psum.tile([P, 512], F32, tag="sum")
+            sum_up(k, bank, (PAIR[1], REST) if k in LEAN else ((0, 1, 2, 3), PAIR[1]))
             if u % 2 == 0:
-                r_new = r_pool.tile([P, 2048], F32)
-                rs[s, u // 2] = r_new
-            r = part(k)
+                z_new = z_pool.tile([P, 2 * 4 * N], F32)
+                zs[s, u // 2] = z_new
             if k in LEAN:
-                am = am_pool.tile([P, N_OUT], F32)
-                nc.scalar.mul(out=am[:], in_=bank[:, 0:N_OUT], mul=1.0 / 16.0)
-                banks[k] = [bank, am]
-                return
-            if u == 0:
-                am = am_pool.tile([P, N_OUT], F32)
+                base = base_pool.tile([P, N], F32)
+                nc.scalar.mul(out=base[:], in_=bank[:, 0:N], mul=1.0 / 16.0)
+                banks[k] = [bank, base[:]]
+            elif u == 0:
+                base = base_pool.tile([P, N], F32)
                 nc.vector.scalar_tensor_tensor(
-                    out=am[:], in0=bank[:, 0:N_OUT], scalar=0.0625, in1=bias_f[:], op0=ALU.mult, op1=ALU.subtract
+                    out=base[:], in0=bank[:, 0:N], scalar=1.0 / 16.0, in1=bias_f[:], op0=ALU.mult, op1=ALU.subtract
                 )
-                banks[k] = [bank, am[:]]
-                return
-            nc.scalar.mul(out=r[:, 0:N_OUT], in_=bank[:, 0:N_OUT], mul=1.0 / 16.0)
-            banks[k] = [bank, r[:, 0:N_OUT]]
+                banks[k] = [bank, base[:]]
+            else:
+                nc.scalar.mul(out=z_of(k)[:, 0:N], in_=bank[:, 0:N], mul=1.0 / 16.0)
+                banks[k] = [bank, z_of(k)[:, 0:N]]
 
-        def sums_y(k):
-            bank = ps_a.tile([P, 512], F32, tag="acc")
-            sums(k, bank, (PLUS[2], PLUS[3]))
+        def second_sums(k):
+            bank = sum_psum.tile([P, 512], F32, tag="sum")
+            sum_up(k, bank, (PAIR[2], PAIR[3]))
             banks[k].append(bank)
 
-        def level1_x(k):
+        def first_z(k):
+            z = z_of(k)
+            bank, base = banks[k]
             if k in LEAN:
-                bank, am = banks[k]
-                for q, sign in ((0, 1.0), (1, -1.0)):
+                for q, factor in ((0, 1.0 / 16.0), (1, -1.0 / 16.0)):
                     nc.vector.scalar_tensor_tensor(
-                        out=part(k)[:, N_OUT * q : N_OUT * q + N_OUT], in0=bank[:, N_OUT:512], scalar=sign / 16.0, in1=am[:],
-                        op0=ALU.mult, op1=ALU.add,
+                        out=z[:, N * q : N * q + N], in0=bank[:, N:512], scalar=factor, in1=base, op0=ALU.mult, op1=ALU.add
                     )
-                base = part(k)[:, 0:N_OUT]
-                banks[k][1] = base
-                return
-            if ORDER[k][1] == 0:
-                bank, base = banks[k][0], banks[k][1]
+                banks[k][1] = z[:, 0:N]
+            elif ORDER[k][1] == 0:
                 nc.vector.scalar_tensor_tensor(
-                    out=halves(part(k)[:, 0:512]), in0=halves(bank[:]), scalar=0.125,
-                    in1=base.unsqueeze(1).to_broadcast([P, 2, N_OUT]), op0=ALU.mult, op1=ALU.subtract,
+                    out=by_two(z[:, 0:512]), in0=by_two(bank[:]), scalar=0.125, in1=twice(base), op0=ALU.mult, op1=ALU.subtract
                 )
-                return
-            nc.vector.scalar_tensor_tensor(
-                out=part(k)[:, N_OUT:512], in0=banks[k][0][:, N_OUT:512], scalar=0.125, in1=banks[k][1],
-                op0=ALU.mult, op1=ALU.subtract,
-            )
+            else:
+                nc.vector.scalar_tensor_tensor(
+                    out=z[:, N:512], in0=bank[:, N:512], scalar=0.125, in1=base, op0=ALU.mult, op1=ALU.subtract
+                )
 
-        def level1_y(k):
+        def second_z(k):
             s, u = ORDER[k]
             nc.vector.scalar_tensor_tensor(
-                out=halves(part(k)[:, 512:1024]), in0=halves(banks[k][2][:]), scalar=0.125,
-                in1=banks[k][1].unsqueeze(1).to_broadcast([P, 2, N_OUT]), op0=ALU.mult, op1=ALU.subtract,
+                out=by_two(z_of(k)[:, 512:1024]), in0=by_two(banks[k][2][:]), scalar=0.125, in1=twice(banks[k][1]),
+                op0=ALU.mult, op1=ALU.subtract,
             )
             if u % 2 == 1:
-                add, sub = [(pair_stage, s, u // 2, op) for op in (ALU.add, ALU.subtract)]
-                rows = [(finish, s, pp) for pp in (0, 2, 1, 3)] if u == 3 else []
-                later.extend([add] + rows[:2] + [sub] + rows[2:] if s == 3 else [add, sub] + rows)
+                plus, minus = [(pair_of_u, s, u // 2, op) for op in (ALU.add, ALU.subtract)]
+                finish = [(output_row, s, row) for row in (0, 2, 1, 3)] if u == 3 else []
+                waiting.extend([plus] + finish[:2] + [minus] + finish[2:] if s == 3 else [plus, minus] + finish)
 
-        def combine(out_tile, lo, in0, lo0, in1, lo1, op):
-            nc.vector.tensor_tensor(
-                out=out_tile[:, lo : lo + 1024], in0=in0[:, lo0 : lo0 + 1024], in1=in1[:, lo1 : lo1 + 1024], op=op
-            )
+        def add(target, a, b, op):
+            nc.vector.tensor_tensor(out=target, in0=a, in1=b, op=op)
 
-        def pair_stage(s, h, op):
+        def pair_of_u(s, h, op):
             if op == ALU.add:
-                z_new = z_pool.tile([P, 2048], F32)
-                zs[s, h] = z_new
-            combine(zs[s, h], 0 if op == ALU.add else 1024, rs[s, h], 0, rs[s, h], 1024, op)
+                half_new = half_pool.tile([P, 2 * 4 * N], F32)
+                halves[s, h] = half_new
+            z = zs[s, h]
+            lo = 0 if op == ALU.add else 1024
+            add(halves[s, h][:, lo : lo + 1024], z[:, 0:1024], z[:, 1024:2048], op)
 
-        def finish(s, pp):
-            if pp < 2:
-                o_new = stage_pool.tile([P, 2048], F32, align_bytes=64, tag="stage")
-                outs[s] = o_new
-            o = outs[s]
-            lo = 1024 * (pp // 2)
-            from_z = 1024 * (pp % 2)
-            combine(o, lo, zs[s, 0], from_z, zs[s, 1], from_z, ALU.add if pp < 2 else ALU.subtract)
-            if s == 3 or pp >= 2:
-                count = 1 if s == 3 else 2
-                first = pp if s == 3 else pp - 2
-                for jj in range(4):
-                    nc.sync.dma_start(
-                        out=o_view[:, first : pp + 1 : 2, jj, s, :],
-                        in_=o[jj:P:4, 1024 * (first // 2) : 1024 * (first // 2) + 1024 * count].rearrange("p (m c) -> p m c", m=count),
-                    )
+        def output_row(s, row):
+            if row < 2:
+                rows_new = stage_pool.tile([P, 2 * 4 * N], F32, align_bytes=64, tag="stage")
+                rows[s] = rows_new
+            lo = 1024 * (row % 2)
+            place = 1024 * (row // 2)
+            add(
+                rows[s][:, place : place + 1024], halves[s, 0][:, lo : lo + 1024], halves[s, 1][:, lo : lo + 1024],
+                ALU.add if row < 2 else ALU.subtract,
+            )
+            if s == 3:
+                first, count = row, 1
+            elif row >= 2:
+                first, count = row - 2, 2
+            else:
+                return
+            begin = 1024 * (first // 2)
+            for jj in range(4):
+                nc.sync.dma_start(
+                    out=o_view[:, first : row + 1 : 2, jj, s, :],
+                    in_=rows[s][jj:P:4, begin : begin + 1024 * count].rearrange("p (m c) -> p m c", m=count),
+                )
 
-        later = []
-
-        def second_level():
-            if later:
-                job = later.pop(0)
+        def sums_over_u():
+            if waiting:
+                job = waiting.pop(0)
                 job[0](*job[1:])
 
-        fill = list(FILL)
+        scalar_halves = [(t, g) for t in SCALAR_T for g in range(2)]
 
-        def filler():
-            code = fill.pop(0) if fill else 0
-            if code > 0:
-                regroup_vector(code)
-            elif code < 0:
-                quantise_w(-code)
-            else:
-                second_level()
+        def regroup_halves(count):
+            for i in range(count):
+                t, g = scalar_halves.pop(0)
+                regroup_on_scalar(t, g)
 
-        loads()
-        turn(0, 0)
-        copy_out(0, 0)
-        turn(0, 1)
-        copy_out(0, 1)
+        def free_place(k, place):
+            work = WEIGHT_WORK.get((k, place))
+            if work is not None:
+                job = regroup if work[0] == "regroup" else quantise
+                job(work[1])
+            elif place != 1 or len(waiting) > WAITING:
+                sums_over_u()
+
+        issue_loads()
+        for half in range(2):
+            transpose(0, half)
+            copy_out(0, half)
         for g in range(2):
-            regroup_scalar(2, g)
-        for code in HEAD:
-            if code == 100:
-                quantise_x(0)
-            elif code == 101:
-                turn(1, 0)
-                copy_out(1, 0)
-            elif code < 0:
-                quantise_w(-code - 10)
-            else:
-                regroup_vector(code)
-        done = {}
-
-        def pieces(ts):
-            for t in ts:
-                done[t] = done.get(t, -1) + 1
-                regroup_scalar(t, done[t])
+            regroup_on_scalar(2, g)
+        regroup(0)
+        regroup(1)
+        quantise_x(0)
+        regroup(3)
+        quantise(0)
+        transpose(1, 0)
+        copy_out(1, 0)
+        quantise(1)
 
         for k in range(STEPS):
             if k + 1 < STEPS:
-                turn(k + 1, 1)
+                transpose(k + 1, 1)
                 copy_out(k + 1, 1)
-            pieces(EARLY.get(k, ()))
+            regroup_halves(HALVES_BETWEEN.get(k, 0))
             if k >= 1:
-                level1_y(k - 1)
-            filler()
+                second_z(k - 1)
+            free_place(k, 0)
             if k + 1 < STEPS:
                 quantise_x(k + 1)
-            sums_x(k)
-            if (fill and fill[0] != 0) or len(later) > THR:
-                filler()
-            elif fill:
-                fill.pop(0)
-            level1_x(k)
+            first_sums(k)
+            free_place(k, 1)
+            first_z(k)
             if k + 2 < STEPS:
-                turn(k + 2, 0)
+                transpose(k + 2, 0)
                 copy_out(k + 2, 0)
-            pieces(LATE.get(k, ()))
-            sums_y(k)
-            filler()
-        level1_y(STEPS - 1)
-        while later:
-            second_level()
+            regroup_halves(HALVES_AFTER.get(k, 0))
+            second_sums(k)
+            free_place(k, 2)
+        second_z(STEPS - 1)
+        while waiting:
+            sums_over_u()

@@ -15,13 +15,13 @@ C = 1024
 N = 256
 FLOPS = 2 * 16 * 512 * C * N
 
-PAIR = {1: (0, 2), 2: (0, 1), 3: (0, 3)}
-REST = (1, 3)
+PAIR = {0: (0, 1, 2, 3), 1: (0, 2), 2: (0, 1), 3: (0, 3)}
+REST = {0: (), 1: (1, 3), 2: (2, 3), 3: (1, 2)}
 
 ORDER = [(s, u) for pair in ((0, 1), (2, 3)) for u in (0, 1) for s in pair] + [(s, u) for s in range(4) for u in (2, 3)]
 STEPS = len(ORDER)
 
-LOADS = [("x", 0, 0, 0), ("x", 0, 1, 0), ("w", 0), ("w", 1), ("w", 2), ("x", 1, 0, 0), ("x", 1, 1, 0), ("w", 3)]
+LOADS = [("step", 0), ("w", 0), ("w", 1), ("step", 1), ("w", 2), ("x", 1, 0, 0), ("x", 1, 1, 0), ("w", 3)]
 FIRST_HALF = [("x", 0, 0, 1), ("x", 0, 1, 1), ("w", 4), ("x", 1, 0, 1), ("w", 5), ("x", 1, 1, 1), ("w", 6), ("w", 7)]
 SECOND_HALF = [("x", u, half, pair) for pair in range(2) for u in (2, 3) for half in range(2)]
 LOAD_BUFFERS = 7
@@ -99,11 +99,15 @@ def tile_iwht3layer_pa_t_kernel(tc, trans, weight, bias, out):
                             in_=w_view[:, 2 * name[1] + i, :, :],
                         )
                 else:
-                    u, half, pair = name[1:]
-                    t = 4 * u + 2 * half
+                    if name[0] == "step":
+                        s, u = ORDER[name[1]]
+                        t, count, first = 4 * u, 4, C * s
+                    else:
+                        u, half, pair = name[1:]
+                        t, count, first = 4 * u + 2 * half, 2, 2 * C * pair
                     nc.sync.dma_start(
-                        out=raw[:].rearrange("p (v m) -> p v m", v=2),
-                        in_=x_view[:, t : t + 2, 2 * C * pair : 2 * C * pair + 2 * C],
+                        out=raw[:].rearrange("p (v m) -> p v m", v=count),
+                        in_=x_view[:, t : t + count, first : first + 4 * C // count],
                     )
 
         def read_once(name):
@@ -118,13 +122,13 @@ def tile_iwht3layer_pa_t_kernel(tc, trans, weight, bias, out):
             if half == 0:
                 xt = turned_pool.tile([P, 4096], BF16, align_bytes=64)
                 turned[k] = xt
-            name = ("x", u, half, s // 2)
+            name = ("step", k) if k < 2 else ("x", u, half, s // 2)
             words = loaded[name][:].bitcast(F32)
             tiles = []
             for v in range(2):
                 bank = turn_psum.tile([P, 512], F32)
                 for g in range(2):
-                    first = 1024 * v + 512 * (s % 2) + 256 * g
+                    first = 256 * g + (512 * (2 * half + v) if k < 2 else 1024 * v + 512 * (s % 2))
                     for e in range(2):
                         lo = P * (2 * g + e)
                         nc.tensor.transpose(bank[:, lo : lo + P], words[:, first + e : first + 256 : 2], ident[:])
@@ -177,23 +181,24 @@ def tile_iwht3layer_pa_t_kernel(tc, trans, weight, bias, out):
                 out=w_codes[:, lo : lo + 1024].bitcast(FP8X4), scales=w_scales[:, lo : lo + 1024], in_=grouped[k][:]
             )
 
-        def sum_up(k, bank, members):
-            u = ORDER[k][1]
-            codes, scales = x_codes[k]
-            for side, vs in enumerate(members):
-                passes = [(v, g) for v in vs for g in range(2)]
-                for i, (v, g) in enumerate(passes):
-                    xo = P * (2 * v + g)
-                    wo = N * (2 * (4 * u + v) + g)
-                    nc.tensor.matmul_mx(
-                        out=bank[:, N * side : N * side + N],
-                        lhsT=codes[:, xo : xo + P].bitcast(FP8X4),
-                        lhsT_scale=scales[:, xo : xo + P],
-                        rhs=w_codes[:, wo : wo + N].bitcast(FP8X4),
-                        rhs_scale=w_scales[:, wo : wo + N],
-                        start=(i == 0),
-                        stop=(i == len(passes) - 1),
-                    )
+        def terms(k, vs):
+            return [(k, v) for v in vs]
+
+        def sum_up(bank, side, members):
+            passes = [(k, v, g) for k, v in members for g in range(2)]
+            for i, (k, v, g) in enumerate(passes):
+                codes, scales = x_codes[k]
+                xo = P * (2 * v + g)
+                wo = N * (2 * (4 * ORDER[k][1] + v) + g)
+                nc.tensor.matmul_mx(
+                    out=bank[:, N * side : N * side + N],
+                    lhsT=codes[:, xo : xo + P].bitcast(FP8X4),
+                    lhsT_scale=scales[:, xo : xo + P],
+                    rhs=w_codes[:, wo : wo + N].bitcast(FP8X4),
+                    rhs_scale=w_scales[:, wo : wo + N],
+                    start=(i == 0),
+                    stop=(i == len(passes) - 1),
+                )
 
         def by_two(ap):
             return ap.rearrange("p (m n) -> p m n", m=2)
@@ -208,7 +213,8 @@ def tile_iwht3layer_pa_t_kernel(tc, trans, weight, bias, out):
         def first_sums(k):
             s, u = ORDER[k]
             bank = sum_psum.tile([P, 512], F32, tag="sum")
-            sum_up(k, bank, (PAIR[1], REST) if k in LEAN else ((0, 1, 2, 3), PAIR[1]))
+            sum_up(bank, 0, terms(k, PAIR[1] if k in LEAN else PAIR[0]))
+            sum_up(bank, 1, terms(k, REST[1] if k in LEAN else PAIR[1]))
             if u % 2 == 0:
                 z_new = z_pool.tile([P, 2 * 4 * N], F32)
                 zs[s, u // 2] = z_new
@@ -228,7 +234,8 @@ def tile_iwht3layer_pa_t_kernel(tc, trans, weight, bias, out):
 
         def second_sums(k):
             bank = sum_psum.tile([P, 512], F32, tag="sum")
-            sum_up(k, bank, (PAIR[2], PAIR[3]))
+            sum_up(bank, 0, terms(k, PAIR[2]))
+            sum_up(bank, 1, terms(k, PAIR[3]))
             banks[k].append(bank)
 
         def first_z(k):
@@ -258,7 +265,7 @@ def tile_iwht3layer_pa_t_kernel(tc, trans, weight, bias, out):
             if u % 2 == 1:
                 plus, minus = [(pair_of_u, s, u // 2, op) for op in (ALU.add, ALU.subtract)]
                 finish = [(output_row, s, row) for row in (0, 2, 1, 3)] if u == 3 else []
-                waiting.extend([plus] + finish[:2] + [minus] + finish[2:] if s == 3 else [plus, minus] + finish)
+                waiting.extend([plus, minus] + finish)
 
         def add(target, a, b, op):
             nc.vector.tensor_tensor(out=target, in0=a, in1=b, op=op)
@@ -281,18 +288,52 @@ def tile_iwht3layer_pa_t_kernel(tc, trans, weight, bias, out):
                 rows[s][:, place : place + 1024], halves[s, 0][:, lo : lo + 1024], halves[s, 1][:, lo : lo + 1024],
                 ALU.add if row < 2 else ALU.subtract,
             )
-            if s == 3:
-                first, count = row, 1
-            elif row >= 2:
-                first, count = row - 2, 2
-            else:
-                return
-            begin = 1024 * (first // 2)
-            for jj in range(4):
-                nc.sync.dma_start(
-                    out=o_view[:, first : row + 1 : 2, jj, s, :],
-                    in_=rows[s][jj:P:4, begin : begin + 1024 * count].rearrange("p (m c) -> p m c", m=count),
+            if row >= 2:
+                for jj in range(4):
+                    nc.sync.dma_start(
+                        out=o_view[:, row - 2 : row + 1 : 2, jj, s, :], in_=rows[s][jj:P:4, :].rearrange("p (m c) -> p m c", m=2)
+                    )
+
+        def last_pair():
+            k2, k3 = STEPS - 2, STEPS - 1
+            s = ORDER[k3][0]
+            differences_01 = sum_psum.tile([P, 512], F32, tag="sum")
+            sums_01 = sum_psum.tile([P, 512], F32, tag="sum")
+            sums_23 = sum_psum.tile([P, 512], F32, tag="sum")
+            differences_23 = sum_psum.tile([P, 512], F32, tag="sum")
+            sum_up(differences_01, 0, terms(k2, PAIR[0]))
+            sum_up(sums_01, 0, terms(k2, PAIR[0]) + terms(k3, PAIR[0]))
+            sum_up(sums_01, 1, terms(k2, PAIR[1]) + terms(k3, PAIR[1]))
+            sum_up(sums_23, 0, terms(k2, PAIR[2]) + terms(k3, PAIR[2]))
+            sum_up(sums_23, 1, terms(k2, PAIR[3]) + terms(k3, PAIR[3]))
+            sum_up(differences_01, 1, terms(k2, PAIR[1]) + terms(k3, REST[1]))
+            sum_up(differences_23, 0, terms(k2, PAIR[2]) + terms(k3, REST[2]))
+            sum_up(differences_23, 1, terms(k2, PAIR[3]) + terms(k3, REST[3]))
+            half_new = half_pool.tile([P, 2 * 4 * N], F32)
+            halves[s, 1] = half_new
+            base = half_new[:, 0:N]
+            nc.scalar.mul(out=base, in_=sums_01[:, 0:N], mul=1.0 / 16.0)
+
+            def less_base(lo, bank):
+                nc.vector.scalar_tensor_tensor(
+                    out=by_two(half_new[:, lo : lo + 512]), in0=by_two(bank[:]), scalar=0.125, in1=twice(base),
+                    op0=ALU.mult, op1=ALU.subtract,
                 )
+
+            while len(waiting) > 2:
+                sums_over_u()
+            nc.vector.scalar_tensor_tensor(
+                out=half_new[:, N:512], in0=sums_01[:, N:512], scalar=0.125, in1=base, op0=ALU.mult, op1=ALU.subtract
+            )
+            while waiting:
+                sums_over_u()
+            less_base(512, sums_23)
+            less_base(1024, differences_01)
+            output_row(s, 0)
+            output_row(s, 2)
+            less_base(1536, differences_23)
+            output_row(s, 1)
+            output_row(s, 3)
 
         def sums_over_u():
             if waiting:
@@ -329,25 +370,23 @@ def tile_iwht3layer_pa_t_kernel(tc, trans, weight, bias, out):
         copy_out(1, 0)
         quantise(1)
 
-        for k in range(STEPS):
-            if k + 1 < STEPS:
-                transpose(k + 1, 1)
-                copy_out(k + 1, 1)
+        for k in range(STEPS - 2):
+            transpose(k + 1, 1)
+            copy_out(k + 1, 1)
             regroup_halves(HALVES_BETWEEN.get(k, 0))
             if k >= 1:
                 second_z(k - 1)
             free_place(k, 0)
-            if k + 1 < STEPS:
-                quantise_x(k + 1)
+            quantise_x(k + 1)
             first_sums(k)
             free_place(k, 1)
             first_z(k)
-            if k + 2 < STEPS:
-                transpose(k + 2, 0)
-                copy_out(k + 2, 0)
+            for half in range(2 if k + 2 == STEPS - 1 else 1):
+                transpose(k + 2, half)
+                copy_out(k + 2, half)
             regroup_halves(HALVES_AFTER.get(k, 0))
             second_sums(k)
             free_place(k, 2)
-        second_z(STEPS - 1)
-        while waiting:
-            sums_over_u()
+        quantise_x(STEPS - 1)
+        second_z(STEPS - 3)
+        last_pair()

@@ -16,7 +16,7 @@ N = 256
 FLOPS = 2 * 16 * 512 * C * N
 
 PAIR = {0: (0, 1, 2, 3), 1: (0, 2), 2: (0, 1), 3: (0, 3)}
-REST = {0: (), 1: (1, 3), 2: (2, 3), 3: (1, 2)}
+REST = {1: (1, 3), 2: (2, 3), 3: (1, 2)}
 
 ORDER = [(s, u) for pair in ((0, 1), (2, 3)) for u in (0, 1) for s in pair] + [(s, u) for s in range(4) for u in (2, 3)]
 STEPS = len(ORDER)
@@ -37,14 +37,14 @@ WEIGHT_WORK = {
 }
 WAITING = 2
 
-LEAN = (2, 3, 6, 7, 8, 9)
+LEAN_STEPS = 10
 
 
 def tile_iwht3layer_pa_t_kernel(tc, trans, weight, bias, out):
     nc = tc.nc
     x_view = trans.rearrange("t b i (jj s) c -> (b i jj) t (s c)", s=4)
-    w_view = weight.rearrange("t (g q j) n -> q t g (j n)", g=2, q=P, j=4)
-    o_view = out.rearrange("b (i pp) (jj s q) n -> (b i) pp jj s (q n)", pp=4, jj=4, s=4, q=4)
+    w_view = weight.rearrange("t (g q j) n -> q (t g) (j n)", g=2, q=P, j=4)
+    o_view = out.rearrange("b (i pp) (jj s q) n -> pp s (b i) jj (q n)", pp=4, jj=4, s=4, q=4)
 
     with ExitStack() as ctx:
         const = ctx.enter_context(tc.tile_pool(name="const", bufs=1))
@@ -62,10 +62,12 @@ def tile_iwht3layer_pa_t_kernel(tc, trans, weight, bias, out):
 
         ident = const.tile([P, P], F32)
         make_identity(nc, ident[:])
-        bias_bf = const.tile([P, N], BF16)
-        nc.scalar.dma_start(out=bias_bf[:], in_=bias.rearrange("a b c n -> (a b c n)").partition_broadcast(P))
+        bias_row = const.tile([P, N], BF16)
+        nc.vector.memset(bias_row[:], 0.0)
+        nc.scalar.dma_start(out=bias_row[0:1, :], in_=bias.rearrange("a b c n -> (a b c) n"))
+        ones = const.tile([P, P], BF16)
+        nc.vector.memset(ones[:], 1.0)
         bias_f = const.tile([P, N], F32)
-        nc.gpsimd.tensor_copy(out=bias_f[:], in_=bias_bf[:])
         w_codes = codes_pool.tile([P, 16 * 2 * N], U32, align_bytes=64)
         w_scales = codes_pool.tile([P, 16 * 2 * N], U8, align_bytes=64)
 
@@ -93,10 +95,11 @@ def tile_iwht3layer_pa_t_kernel(tc, trans, weight, bias, out):
                 raw = load_pool.tile([P, 4096], BF16)
                 loaded[name] = raw
                 if name[0] == "w":
-                    for i in range(2):
+                    count = 2 if name[1] == 0 else 4
+                    for first in range(0, 4, count):
                         nc.sync.dma_start(
-                            out=raw[:, 2048 * i : 2048 * i + 2048].rearrange("q (g m) -> q g m", g=2),
-                            in_=w_view[:, 2 * name[1] + i, :, :],
+                            out=raw[:, 1024 * first : 1024 * (first + count)].rearrange("q (m c) -> q m c", m=count),
+                            in_=w_view[:, 4 * name[1] + first : 4 * name[1] + first + count, :],
                         )
                 else:
                     if name[0] == "step":
@@ -212,56 +215,51 @@ def tile_iwht3layer_pa_t_kernel(tc, trans, weight, bias, out):
 
         def first_sums(k):
             s, u = ORDER[k]
+            lean = k < LEAN_STEPS
             bank = sum_psum.tile([P, 512], F32, tag="sum")
-            sum_up(bank, 0, terms(k, PAIR[1] if k in LEAN else PAIR[0]))
-            sum_up(bank, 1, terms(k, REST[1] if k in LEAN else PAIR[1]))
+            sum_up(bank, 0, terms(k, PAIR[1] if lean else PAIR[0]))
+            sum_up(bank, 1, terms(k, REST[1] if lean else PAIR[1]))
             if u % 2 == 0:
                 z_new = z_pool.tile([P, 2 * 4 * N], F32)
                 zs[s, u // 2] = z_new
-            if k in LEAN:
-                base = base_pool.tile([P, N], F32)
-                nc.scalar.mul(out=base[:], in_=bank[:, 0:N], mul=1.0 / 16.0)
-                banks[k] = [bank, base[:]]
-            elif u == 0:
-                base = base_pool.tile([P, N], F32)
+            base = z_of(k)[:, 0:N]
+            if lean:
+                b_1 = base_pool.tile([P, N], F32)
+                base = b_1[:]
+            if u == 0:
                 nc.vector.scalar_tensor_tensor(
-                    out=base[:], in0=bank[:, 0:N], scalar=1.0 / 16.0, in1=bias_f[:], op0=ALU.mult, op1=ALU.subtract
+                    out=base, in0=bank[:, 0:N], scalar=1.0 / 16.0, in1=bias_f[:], op0=ALU.mult, op1=ALU.add
                 )
-                banks[k] = [bank, base[:]]
             else:
-                nc.scalar.mul(out=z_of(k)[:, 0:N], in_=bank[:, 0:N], mul=1.0 / 16.0)
-                banks[k] = [bank, z_of(k)[:, 0:N]]
+                nc.scalar.mul(out=base, in_=bank[:, 0:N], mul=1.0 / 16.0)
+            banks[k] = [bank, base]
 
         def second_sums(k):
             bank = sum_psum.tile([P, 512], F32, tag="sum")
-            sum_up(bank, 0, terms(k, PAIR[2]))
-            sum_up(bank, 1, terms(k, PAIR[3]))
+            members = REST if ORDER[k][1] == 0 else PAIR
+            sum_up(bank, 0, terms(k, members[2]))
+            sum_up(bank, 1, terms(k, members[3]))
             banks[k].append(bank)
+
+        def z_from(k, target, bank, base):
+            factor, op = (-0.125, ALU.add) if ORDER[k][1] == 0 else (0.125, ALU.subtract)
+            nc.vector.scalar_tensor_tensor(out=target, in0=bank, scalar=factor, in1=base, op0=ALU.mult, op1=op)
 
         def first_z(k):
             z = z_of(k)
             bank, base = banks[k]
-            if k in LEAN:
+            if k < LEAN_STEPS:
                 for q, factor in ((0, 1.0 / 16.0), (1, -1.0 / 16.0)):
                     nc.vector.scalar_tensor_tensor(
                         out=z[:, N * q : N * q + N], in0=bank[:, N:512], scalar=factor, in1=base, op0=ALU.mult, op1=ALU.add
                     )
                 banks[k][1] = z[:, 0:N]
-            elif ORDER[k][1] == 0:
-                nc.vector.scalar_tensor_tensor(
-                    out=by_two(z[:, 0:512]), in0=by_two(bank[:]), scalar=0.125, in1=twice(base), op0=ALU.mult, op1=ALU.subtract
-                )
             else:
-                nc.vector.scalar_tensor_tensor(
-                    out=z[:, N:512], in0=bank[:, N:512], scalar=0.125, in1=base, op0=ALU.mult, op1=ALU.subtract
-                )
+                z_from(k, z[:, N:512], bank[:, N:512], base)
 
         def second_z(k):
             s, u = ORDER[k]
-            nc.vector.scalar_tensor_tensor(
-                out=by_two(z_of(k)[:, 512:1024]), in0=by_two(banks[k][2][:]), scalar=0.125, in1=twice(banks[k][1]),
-                op0=ALU.mult, op1=ALU.subtract,
-            )
+            z_from(k, by_two(z_of(k)[:, 512:1024]), by_two(banks[k][2][:]), twice(banks[k][1]))
             if u % 2 == 1:
                 plus, minus = [(pair_of_u, s, u // 2, op) for op in (ALU.add, ALU.subtract)]
                 finish = [(output_row, s, row) for row in (0, 2, 1, 3)] if u == 3 else []
@@ -288,11 +286,7 @@ def tile_iwht3layer_pa_t_kernel(tc, trans, weight, bias, out):
                 rows[s][:, place : place + 1024], halves[s, 0][:, lo : lo + 1024], halves[s, 1][:, lo : lo + 1024],
                 ALU.add if row < 2 else ALU.subtract,
             )
-            if row >= 2:
-                for jj in range(4):
-                    nc.sync.dma_start(
-                        out=o_view[:, row - 2 : row + 1 : 2, jj, s, :], in_=rows[s][jj:P:4, :].rearrange("p (m c) -> p m c", m=2)
-                    )
+            nc.sync.dma_start(out=o_view[row, s], in_=rows[s][:, place : place + 1024])
 
         def last_pair():
             k2, k3 = STEPS - 2, STEPS - 1
@@ -330,8 +324,8 @@ def tile_iwht3layer_pa_t_kernel(tc, trans, weight, bias, out):
             less_base(512, sums_23)
             less_base(1024, differences_01)
             output_row(s, 0)
-            output_row(s, 2)
             less_base(1536, differences_23)
+            output_row(s, 2)
             output_row(s, 1)
             output_row(s, 3)
 
@@ -368,6 +362,9 @@ def tile_iwht3layer_pa_t_kernel(tc, trans, weight, bias, out):
         quantise(0)
         transpose(1, 0)
         copy_out(1, 0)
+        bias_bank = sum_psum.tile([P, 512], F32, tag="sum")
+        nc.tensor.matmul(bias_bank[:, 0:N], lhsT=ones[:], rhs=bias_row[:], start=True, stop=True)
+        nc.scalar.copy(out=bias_f[:], in_=bias_bank[:, 0:N])
         quantise(1)
 
         for k in range(STEPS - 2):

from contextlib import ExitStack

import concourse.mybir as mybir
from concourse.masks import make_identity

F32 = mybir.dt.float32
BF16 = mybir.dt.bfloat16
U32 = mybir.dt.uint32
U8 = mybir.dt.uint8
FP8X4 = mybir.dt.float8_e4m3fn_x4
ALU = mybir.AluOpType

P = 128
C = 1024
N = 256
FLOPS = 2 * 16 * 512 * C * N

PAIR = {0: (0, 1, 2, 3), 1: (0, 2), 2: (0, 1), 3: (0, 3)}
REST = {1: (1, 3), 2: (2, 3), 3: (1, 2)}

ORDER = [(s, u) for pair in ((0, 1), (2, 3)) for u in (0, 1) for s in pair] + [(s, u) for s in range(4) for u in (2, 3)]
STEPS = len(ORDER)

LOADS = [("step", 0), ("w", 0), ("w", 1), ("step", 1), ("w", 2), ("x", 1, 0, 0), ("x", 1, 1, 0), ("w", 3)]
FIRST_HALF = [("x", 0, 0, 1), ("x", 0, 1, 1), ("w", 4), ("x", 1, 0, 1), ("w", 5), ("x", 1, 1, 1), ("w", 6), ("w", 7)]
SECOND_HALF = [("x", u, half, pair) for pair in range(2) for u in (2, 3) for half in range(2)]
LOAD_BUFFERS = 7

SCALAR_T = (7, 9, 10, 11, 13, 14, 15)
HALVES_BETWEEN = {1: 2, 3: 1, 4: 1, 5: 1, 6: 1, 7: 2}
HALVES_AFTER = {3: 1, 4: 2, 5: 1, 6: 2}

WEIGHT_WORK = {
    (0, 0): ("regroup", 4), (0, 1): ("regroup", 5), (0, 2): ("quantise", 2), (1, 0): ("regroup", 6), (1, 1): ("quantise", 3),
    (3, 0): ("regroup", 8), (4, 1): ("quantise", 4), (5, 1): ("quantise", 5), (6, 0): ("regroup", 12), (7, 1): ("quantise", 6),
    (8, 0): ("quantise", 7),
}
WAITING = 2

LEAN_STEPS = 10


def tile_iwht3layer_pa_t_kernel(tc, trans, weight, bias, out):
    nc = tc.nc
    x_view = trans.rearrange("t b i (jj s) c -> (b i jj) t (s c)", s=4)
    w_view = weight.rearrange("t (g q j) n -> q (t g) (j n)", g=2, q=P, j=4)
    o_view = out.rearrange("b (i pp) (jj s q) n -> pp s (b i) jj (q n)", pp=4, jj=4, s=4, q=4)

    with ExitStack() as ctx:
        const = ctx.enter_context(tc.tile_pool(name="const", bufs=1))
        codes_pool = ctx.enter_context(tc.tile_pool(name="codes", bufs=1))
        load_pool = ctx.enter_context(tc.tile_pool(name="load", bufs=LOAD_BUFFERS))
        stage_pool = ctx.enter_context(tc.tile_pool(name="stage", bufs=4))
        turned_pool = ctx.enter_context(tc.tile_pool(name="turned", bufs=2))
        xq_pool = ctx.enter_context(tc.tile_pool(name="xq", bufs=3))
        z_pool = ctx.enter_context(tc.tile_pool(name="z", bufs=3))
        base_pool = ctx.enter_context(tc.tile_pool(name="base", bufs=2))
        half_pool = ctx.enter_context(tc.tile_pool(name="half", bufs=6))
        turn_psum = ctx.enter_context(tc.psum_pool(name="turn", bufs=4))
        sum_psum = ctx.enter_context(tc.psum_pool(name="sum", bufs=4))
        ctx.enter_context(tc.manual_schedule())

        ident = const.tile([P, P], F32)
        make_identity(nc, ident[:])
        bias_row = const.tile([P, N], BF16)
        nc.vector.memset(bias_row[:], 0.0)
        nc.scalar.dma_start(out=bias_row[0:1, :], in_=bias.rearrange("a b c n -> (a b c) n"))
        ones = const.tile([P, P], BF16)
        nc.vector.memset(ones[:], 1.0)
        bias_f = const.tile([P, N], F32)
        w_codes = codes_pool.tile([P, 16 * 2 * N], U32, align_bytes=64)
        w_scales = codes_pool.tile([P, 16 * 2 * N], U8, align_bytes=64)

        loaded = {}
        readers = {}
        outstanding = []
        spare = [LOAD_BUFFERS]
        to_load = LOADS + FIRST_HALF + SECOND_HALF
        turned = {}
        turned_psum = {}
        x_codes = {}
        grouped = {}
        banks = {}
        zs = {}
        halves = {}
        rows = {}
        waiting = []

        def issue_loads():
            while to_load and spare[0]:
                spare[0] -= 1
                name = to_load.pop(0)
                outstanding.append(name)
                readers[name] = 2
                raw = load_pool.tile([P, 4096], BF16)
                loaded[name] = raw
                if name[0] == "w":
                    count = 2 if name[1] == 0 else 4
                    for first in range(0, 4, count):
                        nc.sync.dma_start(
                            out=raw[:, 1024 * first : 1024 * (first + count)].rearrange("q (m c) -> q m c", m=count),
                            in_=w_view[:, 4 * name[1] + first : 4 * name[1] + first + count, :],
                        )
                else:
                    if name[0] == "step":
                        s, u = ORDER[name[1]]
                        t, count, first = 4 * u, 4, C * s
                    else:
                        u, half, pair = name[1:]
                        t, count, first = 4 * u + 2 * half, 2, 2 * C * pair
                    nc.sync.dma_start(
                        out=raw[:].rearrange("p (v m) -> p v m", v=count),
                        in_=x_view[:, t : t + count, first : first + 4 * C // count],
                    )

        def read_once(name):
            readers[name] -= 1
            while outstanding and readers[outstanding[0]] == 0:
                outstanding.pop(0)
                spare[0] += 1
            issue_loads()

        def transpose(k, half):
            s, u = ORDER[k]
            if half == 0:
                xt = turned_pool.tile([P, 4096], BF16, align_bytes=64)
                turned[k] = xt
            name = ("step", k) if k < 2 else ("x", u, half, s // 2)
            words = loaded[name][:].bitcast(F32)
            tiles = []
            for v in range(2):
                bank = turn_psum.tile([P, 512], F32)
                for g in range(2):
                    first = 256 * g + (512 * (2 * half + v) if k < 2 else 1024 * v + 512 * (s % 2))
                    for e in range(2):
                        lo = P * (2 * g + e)
                        nc.tensor.transpose(bank[:, lo : lo + P], words[:, first + e : first + 256 : 2], ident[:])
                tiles.append((2 * half + v, bank))
            turned_psum[k, half] = tiles
            read_once(name)

        def copy_out(k, half):
            words = turned[k][:].bitcast(F32)
            for v, bank in turned_psum[k, half]:
                nc.scalar.copy(
                    out=words[:, 512 * v : 512 * v + 512].rearrange("q (g r e) -> q g r e", g=2, r=P, e=2),
                    in_=bank[:].rearrange("q (g e r) -> q g r e", g=2, e=2, r=P),
                )

        def quantise_x(k):
            codes = xq_pool.tile([P, 1024], U32, align_bytes=64)
            scales = xq_pool.tile([P, 1024], U8, align_bytes=64)
            nc.vector.quantize_mx(out=codes[:].bitcast(FP8X4), scales=scales[:], in_=turned[k][:])
            x_codes[k] = (codes, scales)

        def regroup_target(t):
            if t // 2 not in grouped:
                pair_tile = stage_pool.tile([P, 4096], BF16, align_bytes=64, tag="stage")
                grouped[t // 2] = pair_tile
            return grouped[t // 2][:, 2048 * (t % 2) : 2048 * (t % 2) + 2048]

        def regroup_source(t):
            return loaded["w", t // 2][:, 2048 * (t % 2) : 2048 * (t % 2) + 2048]

        def regroup_on_scalar(t, g):
            lo = 1024 * g
            nc.scalar.copy(
                out=regroup_target(t)[:, lo : lo + 1024].rearrange("q (c i j) -> q c j i", c=64, i=4, j=4),
                in_=regroup_source(t)[:, lo : lo + 1024].rearrange("q (j c i) -> q c j i", j=4, c=64, i=4),
            )
            if g == 1:
                read_once(("w", t // 2))

        def regroup(t):
            nc.vector.tensor_copy(
                out=regroup_target(t).rearrange("q (g c i j) -> q g c j i", g=2, c=64, i=4, j=4),
                in_=regroup_source(t).rearrange("q (g j c i) -> q g c j i", g=2, j=4, c=64, i=4),
            )
            read_once(("w", t // 2))

        def quantise(k):
            lo = 1024 * k
            nc.vector.quantize_mx(
                out=w_codes[:, lo : lo + 1024].bitcast(FP8X4), scales=w_scales[:, lo : lo + 1024], in_=grouped[k][:]
            )

        def terms(k, vs):
            return [(k, v) for v in vs]

        def sum_up(bank, side, members):
            passes = [(k, v, g) for k, v in members for g in range(2)]
            for i, (k, v, g) in enumerate(passes):
                codes, scales = x_codes[k]
                xo = P * (2 * v + g)
                wo = N * (2 * (4 * ORDER[k][1] + v) + g)
                nc.tensor.matmul_mx(
                    out=bank[:, N * side : N * side + N],
                    lhsT=codes[:, xo : xo + P].bitcast(FP8X4),
                    lhsT_scale=scales[:, xo : xo + P],
                    rhs=w_codes[:, wo : wo + N].bitcast(FP8X4),
                    rhs_scale=w_scales[:, wo : wo + N],
                    start=(i == 0),
                    stop=(i == len(passes) - 1),
                )

        def by_two(ap):
            return ap.rearrange("p (m n) -> p m n", m=2)

        def twice(ap):
            return ap.unsqueeze(1).to_broadcast([P, 2, N])

        def z_of(k):
            s, u = ORDER[k]
            return zs[s, u // 2][:, 4 * N * (u % 2) : 4 * N * (u % 2) + 4 * N]

        def first_sums(k):
            s, u = ORDER[k]
            lean = k < LEAN_STEPS
            bank = sum_psum.tile([P, 512], F32, tag="sum")
            sum_up(bank, 0, terms(k, PAIR[1] if lean else PAIR[0]))
            sum_up(bank, 1, terms(k, REST[1] if lean else PAIR[1]))
            if u % 2 == 0:
                z_new = z_pool.tile([P, 2 * 4 * N], F32)
                zs[s, u // 2] = z_new
            base = z_of(k)[:, 0:N]
            if lean:
                b_1 = base_pool.tile([P, N], F32)
                base = b_1[:]
            if u == 0:
                nc.vector.scalar_tensor_tensor(
                    out=base, in0=bank[:, 0:N], scalar=1.0 / 16.0, in1=bias_f[:], op0=ALU.mult, op1=ALU.add
                )
            else:
                nc.scalar.mul(out=base, in_=bank[:, 0:N], mul=1.0 / 16.0)
            banks[k] = [bank, base]

        def second_sums(k):
            bank = sum_psum.tile([P, 512], F32, tag="sum")
            members = REST if ORDER[k][1] == 0 else PAIR
            sum_up(bank, 0, terms(k, members[2]))
            sum_up(bank, 1, terms(k, members[3]))
            banks[k].append(bank)

        def z_from(k, target, bank, base):
            factor, op = (-0.125, ALU.add) if ORDER[k][1] == 0 else (0.125, ALU.subtract)
            nc.vector.scalar_tensor_tensor(out=target, in0=bank, scalar=factor, in1=base, op0=ALU.mult, op1=op)

        def first_z(k):
            z = z_of(k)
            bank, base = banks[k]
            if k < LEAN_STEPS:
                for q, factor in ((0, 1.0 / 16.0), (1, -1.0 / 16.0)):
                    nc.vector.scalar_tensor_tensor(
                        out=z[:, N * q : N * q + N], in0=bank[:, N:512], scalar=factor, in1=base, op0=ALU.mult, op1=ALU.add
                    )
                banks[k][1] = z[:, 0:N]
            else:
                z_from(k, z[:, N:512], bank[:, N:512], base)

        def second_z(k):
            s, u = ORDER[k]
            z_from(k, by_two(z_of(k)[:, 512:1024]), by_two(banks[k][2][:]), twice(banks[k][1]))
            if u % 2 == 1:
                plus, minus = [(pair_of_u, s, u // 2, op) for op in (ALU.add, ALU.subtract)]
                finish = [(output_row, s, row) for row in (0, 2, 1, 3)] if u == 3 else []
                waiting.extend([plus, minus] + finish)

        def add(target, a, b, op):
            nc.vector.tensor_tensor(out=target, in0=a, in1=b, op=op)

        def pair_of_u(s, h, op):
            if op == ALU.add:
                half_new = half_pool.tile([P, 2 * 4 * N], F32)
                halves[s, h] = half_new
            z = zs[s, h]
            lo = 0 if op == ALU.add else 1024
            add(halves[s, h][:, lo : lo + 1024], z[:, 0:1024], z[:, 1024:2048], op)

        def output_row(s, row):
            if row < 2:
                rows_new = stage_pool.tile([P, 2 * 4 * N], F32, align_bytes=64, tag="stage")
                rows[s] = rows_new
            lo = 1024 * (row % 2)
            place = 1024 * (row // 2)
            add(
                rows[s][:, place : place + 1024], halves[s, 0][:, lo : lo + 1024], halves[s, 1][:, lo : lo + 1024],
                ALU.add if row < 2 else ALU.subtract,
            )
            nc.sync.dma_start(out=o_view[row, s], in_=rows[s][:, place : place + 1024])

        def last_pair():
            k2, k3 = STEPS - 2, STEPS - 1
            s = ORDER[k3][0]
            differences_01 = sum_psum.tile([P, 512], F32, tag="sum")
            sums_01 = sum_psum.tile([P, 512], F32, tag="sum")
            sums_23 = sum_psum.tile([P, 512], F32, tag="sum")
            differences_23 = sum_psum.tile([P, 512], F32, tag="sum")
            sum_up(differences_01, 0, terms(k2, PAIR[0]))
            sum_up(sums_01, 0, terms(k2, PAIR[0]) + terms(k3, PAIR[0]))
            sum_up(sums_01, 1, terms(k2, PAIR[1]) + terms(k3, PAIR[1]))
            sum_up(sums_23, 0, terms(k2, PAIR[2]) + terms(k3, PAIR[2]))
            sum_up(sums_23, 1, terms(k2, PAIR[3]) + terms(k3, PAIR[3]))
            sum_up(differences_01, 1, terms(k2, PAIR[1]) + terms(k3, REST[1]))
            sum_up(differences_23, 0, terms(k2, PAIR[2]) + terms(k3, REST[2]))
            sum_up(differences_23, 1, terms(k2, PAIR[3]) + terms(k3, REST[3]))
            half_new = half_pool.tile([P, 2 * 4 * N], F32)
            halves[s, 1] = half_new
            base = half_new[:, 0:N]
            nc.scalar.mul(out=base, in_=sums_01[:, 0:N], mul=1.0 / 16.0)

            def less_base(lo, bank):
                nc.vector.scalar_tensor_tensor(
                    out=by_two(half_new[:, lo : lo + 512]), in0=by_two(bank[:]), scalar=0.125, in1=twice(base),
                    op0=ALU.mult, op1=ALU.subtract,
                )

            while len(waiting) > 2:
                sums_over_u()
            nc.vector.scalar_tensor_tensor(
                out=half_new[:, N:512], in0=sums_01[:, N:512], scalar=0.125, in1=base, op0=ALU.mult, op1=ALU.subtract
            )
            while waiting:
                sums_over_u()
            less_base(512, sums_23)
            less_base(1024, differences_01)
            output_row(s, 0)
            less_base(1536, differences_23)
            output_row(s, 2)
            output_row(s, 1)
            output_row(s, 3)

        def sums_over_u():
            if waiting:
                job = waiting.pop(0)
                job[0](*job[1:])

        scalar_halves = [(t, g) for t in SCALAR_T for g in range(2)]

        def regroup_halves(count):
            for i in range(count):
                t, g = scalar_halves.pop(0)
                regroup_on_scalar(t, g)

        def free_place(k, place):
            work = WEIGHT_WORK.get((k, place))
            if work is not None:
                job = regroup if work[0] == "regroup" else quantise
                job(work[1])
            elif place != 1 or len(waiting) > WAITING:
                sums_over_u()

        issue_loads()
        for half in range(2):
            transpose(0, half)
            copy_out(0, half)
        for g in range(2):
            regroup_on_scalar(2, g)
        regroup(0)
        regroup(1)
        quantise_x(0)
        regroup(3)
        quantise(0)
        transpose(1, 0)
        copy_out(1, 0)
        bias_bank = sum_psum.tile([P, 512], F32, tag="sum")
        nc.tensor.matmul(bias_bank[:, 0:N], lhsT=ones[:], rhs=bias_row[:], start=True, stop=True)
        nc.scalar.copy(out=bias_f[:], in_=bias_bank[:, 0:N])
        quantise(1)

        for k in range(STEPS - 2):
            transpose(k + 1, 1)
            copy_out(k + 1, 1)
            regroup_halves(HALVES_BETWEEN.get(k, 0))
            if k >= 1:
                second_z(k - 1)
            free_place(k, 0)
            quantise_x(k + 1)
            first_sums(k)
            free_place(k, 1)
            first_z(k)
            for half in range(2 if k + 2 == STEPS - 1 else 1):
                transpose(k + 2, half)
                copy_out(k + 2, half)
            regroup_halves(HALVES_AFTER.get(k, 0))
            second_sums(k)
            free_place(k, 2)
        quantise_x(STEPS - 1)
        second_z(STEPS - 3)
        last_pair()
